import numpy as np
import ml_dtypes


def mxq(x, axis, fmt="e4m3"):
    dtype, down = {"e4m3": (ml_dtypes.float8_e4m3fn, 7), "e5m2": (ml_dtypes.float8_e5m2, 14)}[fmt]
    v = np.moveaxis(np.asarray(x, np.float32).astype(ml_dtypes.bfloat16).astype(np.float64), axis, -1)
    blocks = v.reshape(v.shape[:-1] + (-1, 32))
    amax = np.abs(blocks).max(-1, keepdims=True)
    byte = np.maximum(np.where(amax > 0, np.frexp(amax)[1] - 1 + 127, 0) - down, 1)
    scale = np.exp2(byte - 127.0)
    codes = (blocks / scale).astype(np.float32).astype(dtype).astype(np.float64)
    return np.moveaxis((codes * scale).reshape(v.shape), -1, axis)


WIDE = False


def mx_kscale(k):
    if not WIDE:
        return np.ones(k)
    levels = np.array([10, -10, 5, -5, 0])
    a = np.random.permutation(np.resize(levels, k // 512 * 4)).reshape(k // 512, 4)
    idx = np.arange(k)
    return np.exp2(a[idx // 512, idx % 128 // 32])


BF16 = ml_dtypes.bfloat16


def bf(x):
    return np.asarray(x, np.float32).astype(BF16)


def f64(x):
    return np.asarray(x).astype(np.float64)


T, B, H, DH, R, L = 128, 2, 16, 128, 64, 512
M = H * DH


def rope_tables():
    inv_freq = 1.0 / (10000.0 ** (f64(np.arange(0, R, 2)) / R))
    pos = f64(np.arange(L))
    ang = pos[:, None] * inv_freq[None, :]
    sin = np.repeat(np.sin(ang), 2, axis=-1)[-T:]
    cos = np.repeat(np.cos(ang), 2, axis=-1)[-T:]
    return sin[:, None, None, :], cos[:, None, None, :]


def rotate_every_two(u):
    return np.stack((-u[..., 1::2], u[..., ::2]), axis=-1).reshape(u.shape)


def apply_rope(u):
    sin, cos = rope_tables()
    u_rot = u[..., :R]
    u_pass = u[..., R:]
    u_rot = u_rot * cos + rotate_every_two(u_rot) * sin
    return np.concatenate([u_rot, u_pass], axis=-1)


def setup_inputs():
    s = mx_kscale(M)
    return {"x": bf(np.random.standard_normal((T, B, M)) * s),
            "in_proj_weight": bf(np.random.standard_normal((3 * M, M)) / np.sqrt(M) / s[None, :]),
            "in_proj_bias": bf(np.random.standard_normal(3 * M) * 0.3)}


def reference(x, in_proj_weight, in_proj_bias):
    all_out = (mxq(f64(x), 2, "e4m3") @ mxq(f64(in_proj_weight), 1, "e4m3").T) + f64(in_proj_bias)
    q, k, v = np.split(all_out, 3, axis=-1)
    qh = q.reshape(T, B, H, DH)
    kh = k.reshape(T, B, H, DH)
    vh = v.reshape(T, B, H, DH)
    return apply_rope(qh), apply_rope(kh), vh

@@ -1,0 +1,287 @@
+import math
+from contextlib import ExitStack
+
+import concourse.mybir as mybir
+from concourse.masks import make_identity
+
+F32 = mybir.dt.float32
+BF16 = mybir.dt.bfloat16
+I32 = mybir.dt.int32
+U32 = mybir.dt.uint32
+U8 = mybir.dt.uint8
+FP8X4 = mybir.dt.float8_e4m3fn_x4
+ALU = mybir.AluOpType
+
+P = 128
+B = 2
+HEADS = 16
+DH = 128
+WIDTH = HEADS * DH
+PAIRS = 32
+HALF = DH // 2
+FIRST_POSITION = 512 - 128
+K_PASS = 4 * P
+PASSES = WIDTH // K_PASS
+WORDS_PASS = K_PASS // 2
+N_TILE = 512
+TILE_HEADS = N_TILE // DH
+PART_TILES = WIDTH // N_TILE
+N_TILES = 3 * PART_TILES
+W_BUFS = 5
+GROUPED_BUFS = 6
+TURN_BANKS = 6
+DOUBLINGS = 5
+ROUND_MAGIC = 1.5 * 2.0**23
+
+FLOPS = 2 * P * B * 3 * WIDTH * WIDTH
+
+
+def turn_four_blocks(nc, banks, ident, block, grouped_words):
+    bank = banks.tile([P, 2, 2, P], F32, tag="bank")
+    for u in range(2):
+        for s in range(2):
+            nc.tensor.transpose(bank[:, u, s, :], block(u, s), ident[:])
+    nc.scalar.copy(out=grouped_words, in_=bank[:].rearrange("p u s r -> p (s r) u"))
+
+
+def tile_multiheadattention_pa_kernel(tc, x, in_proj_weight, in_proj_bias, out_0, out_1, out_2):
+    nc = tc.nc
+    outs = [out_0, out_1, out_2]
+    order = [part * PART_TILES + m for m in range(PART_TILES) for part in range(3)]
+    w_tiles = in_proj_weight.rearrange("(n s p e) k -> n p s e k", s=2, p=P, e=2)
+
+    with ExitStack() as ctx:
+        ctx.enter_context(tc.manual_schedule())
+        const = ctx.enter_context(tc.tile_pool(name="const", bufs=1))
+        w_pool = ctx.enter_context(tc.tile_pool(name="w_pool", bufs=W_BUFS))
+        grouped_pool = ctx.enter_context(tc.tile_pool(name="grouped_pool", bufs=GROUPED_BUFS))
+        mx_pool = ctx.enter_context(tc.tile_pool(name="mx_pool", bufs=2))
+        rope_pool = ctx.enter_context(tc.tile_pool(name="rope_pool", bufs=2))
+        out_pool = ctx.enter_context(tc.tile_pool(name="out_pool", bufs=N_TILES))
+        banks = ctx.enter_context(tc.psum_pool(name="banks", bufs=TURN_BANKS))
+        sums_pool = ctx.enter_context(tc.psum_pool(name="sums_pool", bufs=B))
+
+        w_raw = {}
+        w_grouped = {}
+        w_mx = {}
+        sums = {}
+        results = {}
+        unrotated = {}
+
+        def load_weights(j):
+            raw = w_pool.tile([P, 2, 2, WIDTH], BF16)
+            nc.sync.dma_start(out=raw[:], in_=w_tiles[order[j]])
+            w_raw[j] = raw
+
+        bias_rows = const.tile([P, N_TILE], BF16)
+        nc.vector.memset(bias_rows[:], 0.0)
+        nc.sync.dma_start(out=bias_rows[0:N_TILES, :], in_=in_proj_bias.rearrange("(m c) -> m c", c=N_TILE))
+        x_raw = const.tile([P, B, WIDTH], BF16)
+        nc.sync.dma_start(out=x_raw[:], in_=x)
+        for j in range(W_BUFS):
+            load_weights(j)
+
+        position_int = const.tile([P, 1], I32)
+        nc.gpsimd.iota(position_int[:], pattern=[[0, 1]], base=FIRST_POSITION, channel_multiplier=1)
+        ident = const.tile([P, P], F32)
+        make_identity(nc, ident[:])
+
+        frequency = const.tile([P, PAIRS], F32)
+        nc.vector.memset(frequency[:, 0:1], 1.0)
+        for level in range(DOUBLINGS):
+            run = 2**level
+            nc.vector.tensor_scalar(
+                out=frequency[:, run : 2 * run],
+                in0=frequency[:, 0:run],
+                scalar1=10000.0 ** (-2.0 * run / (2 * PAIRS)),
+                scalar2=None,
+                op0=ALU.mult,
+            )
+        position = const.tile([P, 1], F32)
+        nc.vector.tensor_copy(out=position[:], in_=position_int[:])
+        ident_bf16 = const.tile([P, P], BF16)
+        nc.vector.tensor_copy(out=ident_bf16[:], in_=ident[:])
+        turns = const.tile([P, 2, PAIRS], F32)
+        nc.vector.tensor_scalar(
+            out=turns[:, 0, :],
+            in0=frequency[:],
+            scalar1=position[:, 0:1],
+            scalar2=1.0 / (2.0 * math.pi),
+            op0=ALU.mult,
+            op1=ALU.mult,
+        )
+        nc.vector.tensor_scalar(out=turns[:, 1, :], in0=turns[:, 0, :], scalar1=0.25, scalar2=None, op0=ALU.add)
+        whole_turns = const.tile([P, 2, PAIRS], F32)
+        nc.vector.tensor_scalar(
+            out=whole_turns[:],
+            in0=turns[:],
+            scalar1=ROUND_MAGIC,
+            scalar2=ROUND_MAGIC,
+            op0=ALU.add,
+            op1=ALU.subtract,
+        )
+        part_turns = const.tile([P, 2, PAIRS], F32)
+        nc.vector.tensor_tensor(out=part_turns[:], in0=turns[:], in1=whole_turns[:], op=ALU.subtract)
+        sin_cos = const.tile([P, 2, PAIRS], F32)
+        nc.scalar.activation(
+            out=sin_cos[:], in_=part_turns[:], func=mybir.ActivationFunctionType.Sin, scale=2.0 * math.pi
+        )
+        sin = sin_cos[:, 0, :]
+        cos = sin_cos[:, 1, :]
+
+        bias_all = const.tile([P, 3 * WIDTH], BF16)
+        for pair in range(N_TILES // 2):
+            spread = banks.tile([P, 2 * N_TILE], BF16, tag="bank")
+            for c in range(2):
+                m = 2 * pair + c
+                nc.tensor.matmul(
+                    out=spread[:, c * N_TILE : (c + 1) * N_TILE],
+                    lhsT=ident_bf16[:, m : m + 1].to_broadcast([P, P]),
+                    rhs=bias_rows[:],
+                    start=True,
+                    stop=True,
+                )
+            nc.vector.tensor_copy(out=bias_all[:, 2 * pair * N_TILE : 2 * (pair + 1) * N_TILE], in_=spread[:])
+        minus_sin = const.tile([P, PAIRS], F32)
+        nc.vector.tensor_scalar(out=minus_sin[:], in0=sin, scalar1=-1.0, scalar2=None, op0=ALU.mult)
+
+        x_words = x_raw[:].bitcast(F32)
+        x_grouped = const.tile([P, PASSES, B * P, 4], BF16, align_bytes=64)
+        for g in range(PASSES):
+            turn_four_blocks(
+                nc,
+                banks,
+                ident,
+                lambda u, b: x_words[:, b, g * WORDS_PASS + u * P : g * WORDS_PASS + (u + 1) * P],
+                x_grouped[:, g].bitcast(F32),
+            )
+        x_codes = const.tile([P, PASSES, B * P], U32, align_bytes=64)
+        x_scales = const.tile([P, PASSES, B * P], U8, align_bytes=64)
+        nc.vector.quantize_mx(
+            out=x_codes[:].rearrange("p g c -> p (g c)").bitcast(FP8X4),
+            scales=x_scales[:].rearrange("p g c -> p (g c)"),
+            in_=x_grouped[:].rearrange("p g c t -> p (g c t)"),
+        )
+
+        def turn_weights(j):
+            w_words = w_raw[j][:].bitcast(F32)
+            w_grouped[j] = []
+            for g in range(PASSES):
+                grouped = grouped_pool.tile([P, N_TILE, 4], BF16, align_bytes=64)
+                for e in range(2):
+                    turn_four_blocks(
+                        nc,
+                        banks,
+                        ident,
+                        lambda u, s: w_words[:, s, e, g * WORDS_PASS + u * P : g * WORDS_PASS + (u + 1) * P],
+                        grouped[:].bitcast(F32)[:, e * 2 * P : (e + 1) * 2 * P, :],
+                    )
+                w_grouped[j].append(grouped)
+
+        def quantise_weights(j):
+            codes = mx_pool.tile([P, PASSES, N_TILE], U32, align_bytes=64)
+            scales = mx_pool.tile([P, PASSES, N_TILE], U8, align_bytes=64)
+            for g in range(PASSES):
+                nc.vector.quantize_mx(
+                    out=codes[:, g, :].bitcast(FP8X4),
+                    scales=scales[:, g, :],
+                    in_=w_grouped[j][g][:].rearrange("p c t -> p (c t)"),
+                )
+            w_mx[j] = (codes, scales)
+
+        def multiply(j):
+            codes, scales = w_mx[j]
+            sums[j] = []
+            for b in range(B):
+                total = sums_pool.tile([P, N_TILE], F32)
+                for g in range(PASSES):
+                    nc.tensor.matmul_mx(
+                        out=total[:],
+                        lhsT=x_codes[:, g, b * P : (b + 1) * P].bitcast(FP8X4),
+                        lhsT_scale=x_scales[:, g, b * P : (b + 1) * P],
+                        rhs=codes[:, g, :].bitcast(FP8X4),
+                        rhs_scale=scales[:, g, :],
+                        start=(g == 0),
+                        stop=(g == PASSES - 1),
+                    )
+                sums[j].append(total)
+
+        def add_bias(j):
+            n = order[j]
+            rotated = n < 2 * PART_TILES
+            first_plain = PAIRS if rotated else 0
+            bias = bias_all[:, n * N_TILE : (n + 1) * N_TILE]
+            result = out_pool.tile([P, B, TILE_HEADS, DH], F32)
+            results[j] = result
+            if rotated:
+                halves = rope_pool.tile([P, B, 2, TILE_HEADS, PAIRS], F32)
+                unrotated[j] = halves
+            for b in range(B):
+                total = sums[j][b]
+                nc.vector.tensor_tensor(
+                    out=result[:, b].rearrange("p h (i e) -> p h i e", e=2)[:, :, first_plain:HALF, :],
+                    in0=total[:].rearrange("p (e h i) -> p h i e", e=2, h=TILE_HEADS)[:, :, first_plain:HALF, :],
+                    in1=bias.rearrange("p (h i e) -> p h i e", h=TILE_HEADS, e=2)[:, :, first_plain:HALF, :],
+                    op=ALU.add,
+                )
+                if rotated:
+                    nc.vector.tensor_tensor(
+                        out=halves[:, b],
+                        in0=total[:].rearrange("p (e h i) -> p e h i", e=2, h=TILE_HEADS)[:, :, :, 0:PAIRS],
+                        in1=bias.rearrange("p (h i e) -> p e h i", h=TILE_HEADS, e=2)[:, :, :, 0:PAIRS],
+                        op=ALU.add,
+                    )
+
+        def rotate(j):
+            if j not in unrotated:
+                return
+            halves = unrotated[j]
+            result = results[j]
+            by_cos = rope_pool.tile([P, B, 2, TILE_HEADS, PAIRS], F32)
+            by_sin = rope_pool.tile([P, B, 2, TILE_HEADS, PAIRS], F32)
+            nc.vector.tensor_tensor(
+                out=by_cos[:].rearrange("p b e h i -> p (b e h) i"),
+                in0=halves[:].rearrange("p b e h i -> p (b e h) i"),
+                in1=cos.unsqueeze(1).to_broadcast([P, B * 2 * TILE_HEADS, PAIRS]),
+                op=ALU.mult,
+            )
+            for e, factor in ((0, minus_sin[:]), (1, sin)):
+                nc.vector.tensor_tensor(
+                    out=by_sin[:, :, e],
+                    in0=halves[:, :, 1 - e],
+                    in1=factor.unsqueeze(1).unsqueeze(1).to_broadcast([P, B, TILE_HEADS, PAIRS]),
+                    op=ALU.mult,
+                )
+            for b in range(B):
+                nc.vector.tensor_tensor(
+                    out=result[:, b].rearrange("p h (i e) -> p h i e", e=2)[:, :, 0:PAIRS, :],
+                    in0=by_cos[:, b].rearrange("p e h i -> p h i e"),
+                    in1=by_sin[:, b].rearrange("p e h i -> p h i e"),
+                    op=ALU.add,
+                )
+
+        def store(j):
+            n = order[j]
+            first_head = (n % PART_TILES) * TILE_HEADS
+            nc.sync.dma_start(
+                out=outs[n // PART_TILES][:, :, first_head : first_head + TILE_HEADS, :], in_=results[j][:]
+            )
+
+        waiting = []
+        for j in range(N_TILES + 1):
+            if j < N_TILES:
+                turn_weights(j)
+                if j + W_BUFS < N_TILES:
+                    load_weights(j + W_BUFS)
+            if j > 0:
+                multiply(j - 1)
+            if j < N_TILES:
+                quantise_weights(j)
+            if j > 0:
+                add_bias(j - 1)
+                rotate(j - 1)
+                waiting.append(j - 1)
+                if j + W_BUFS >= N_TILES - 1:
+                    for finished in waiting:
+                        store(finished)
+                    waiting = []

@@ -18,7 +18,6 @@ HEADS = 16
 DH = 128
 WIDTH = HEADS * DH
 PAIRS = 32
-HALF = DH // 2
 FIRST_POSITION = 512 - 128
 K_PASS = 4 * P
 PASSES = WIDTH // K_PASS
@@ -66,7 +65,6 @@ def tile_multiheadattention_pa_kernel(tc, x, in_proj_weight, in_proj_bias, out_0
         w_mx = {}
         sums = {}
         results = {}
-        unrotated = {}
 
         def load_weights(j):
             raw = w_pool.tile([P, 2, 2, WIDTH], BF16)
@@ -142,8 +140,11 @@ def tile_multiheadattention_pa_kernel(tc, x, in_proj_weight, in_proj_bias, out_0
                     stop=True,
                 )
             nc.vector.tensor_copy(out=bias_all[:, 2 * pair * N_TILE : 2 * (pair + 1) * N_TILE], in_=spread[:])
-        minus_sin = const.tile([P, PAIRS], F32)
-        nc.vector.tensor_scalar(out=minus_sin[:], in0=sin, scalar1=-1.0, scalar2=None, op0=ALU.mult)
+        own_factor = const.tile([P, PAIRS, 2], F32)
+        partner_factor = const.tile([P, PAIRS, 2], F32)
+        nc.vector.tensor_copy(out=own_factor[:], in_=cos.unsqueeze(2).to_broadcast([P, PAIRS, 2]))
+        nc.vector.tensor_scalar(out=partner_factor[:, :, 0], in0=sin, scalar1=-1.0, scalar2=None, op0=ALU.mult)
+        nc.vector.tensor_copy(out=partner_factor[:, :, 1], in_=sin)
 
         x_words = x_raw[:].bitcast(F32)
         x_grouped = const.tile([P, PASSES, B * P, 4], BF16, align_bytes=64)
@@ -208,57 +209,42 @@ def tile_multiheadattention_pa_kernel(tc, x, in_proj_weight, in_proj_bias, out_0
 
         def add_bias(j):
             n = order[j]
-            rotated = n < 2 * PART_TILES
-            first_plain = PAIRS if rotated else 0
             bias = bias_all[:, n * N_TILE : (n + 1) * N_TILE]
             result = out_pool.tile([P, B, TILE_HEADS, DH], F32)
             results[j] = result
-            if rotated:
-                halves = rope_pool.tile([P, B, 2, TILE_HEADS, PAIRS], F32)
-                unrotated[j] = halves
             for b in range(B):
-                total = sums[j][b]
                 nc.vector.tensor_tensor(
-                    out=result[:, b].rearrange("p h (i e) -> p h i e", e=2)[:, :, first_plain:HALF, :],
-                    in0=total[:].rearrange("p (e h i) -> p h i e", e=2, h=TILE_HEADS)[:, :, first_plain:HALF, :],
-                    in1=bias.rearrange("p (h i e) -> p h i e", h=TILE_HEADS, e=2)[:, :, first_plain:HALF, :],
+                    out=result[:, b].rearrange("p h (i e) -> p (h i) e", e=2),
+                    in0=sums[j][b][:].rearrange("p (e c) -> p c e", e=2),
+                    in1=bias.rearrange("p (c e) -> p c e", e=2),
                     op=ALU.add,
                 )
-                if rotated:
-                    nc.vector.tensor_tensor(
-                        out=halves[:, b],
-                        in0=total[:].rearrange("p (e h i) -> p e h i", e=2, h=TILE_HEADS)[:, :, :, 0:PAIRS],
-                        in1=bias.rearrange("p (h i e) -> p e h i", h=TILE_HEADS, e=2)[:, :, :, 0:PAIRS],
-                        op=ALU.add,
-                    )
 
         def rotate(j):
-            if j not in unrotated:
+            if order[j] >= 2 * PART_TILES:
                 return
-            halves = unrotated[j]
-            result = results[j]
-            by_cos = rope_pool.tile([P, B, 2, TILE_HEADS, PAIRS], F32)
-            by_sin = rope_pool.tile([P, B, 2, TILE_HEADS, PAIRS], F32)
+            rotated = results[j][:].rearrange("p b h d -> p (b h) d")[:, :, 0 : 2 * PAIRS]
+            channels = rotated.rearrange("p c (i e) -> p c i e", e=2)
+            own = rope_pool.tile([P, B * TILE_HEADS, PAIRS, 2], F32)
+            partner = rope_pool.tile([P, B * TILE_HEADS, PAIRS, 2], F32)
             nc.vector.tensor_tensor(
-                out=by_cos[:].rearrange("p b e h i -> p (b e h) i"),
-                in0=halves[:].rearrange("p b e h i -> p (b e h) i"),
-                in1=cos.unsqueeze(1).to_broadcast([P, B * 2 * TILE_HEADS, PAIRS]),
+                out=own[:],
+                in0=channels,
+                in1=own_factor[:].unsqueeze(1).to_broadcast([P, B * TILE_HEADS, PAIRS, 2]),
                 op=ALU.mult,
             )
-            for e, factor in ((0, minus_sin[:]), (1, sin)):
-                nc.vector.tensor_tensor(
-                    out=by_sin[:, :, e],
-                    in0=halves[:, :, 1 - e],
-                    in1=factor.unsqueeze(1).unsqueeze(1).to_broadcast([P, B, TILE_HEADS, PAIRS]),
-                    op=ALU.mult,
-                )
-            for b in range(B):
-                nc.vector.tensor_tensor(
-                    out=result[:, b].rearrange("p h (i e) -> p h i e", e=2)[:, :, 0:PAIRS, :],
-                    in0=by_cos[:, b].rearrange("p e h i -> p h i e"),
-                    in1=by_sin[:, b].rearrange("p e h i -> p h i e"),
-                    op=ALU.add,
-                )
+            nc.vector.tensor_tensor(
+                out=partner[:],
+                in0=channels[:, :, :, ::-1],
+                in1=partner_factor[:].unsqueeze(1).to_broadcast([P, B * TILE_HEADS, PAIRS, 2]),
+                op=ALU.mult,
+            )
+            nc.vector.tensor_tensor(
+                out=rotated,
+                in0=own[:].rearrange("p c i e -> p c (i e)"),
+                in1=partner[:].rearrange("p c i e -> p c (i e)"),
+                op=ALU.add,
+            )
 
         def store(j):
             n = order[j]

@@ -27,7 +27,10 @@ TILE_HEADS = N_TILE // DH
 PART_TILES = WIDTH // N_TILE
 N_TILES = 3 * PART_TILES
 W_BUFS = 5
-GROUPED_BUFS = 6
+GROUPED_BUFS = 8
+BIAS_ROWS = 4
+EARLY_SPREADS = 2
+SPLIT_TILES = 3
 TURN_BANKS = 6
 DOUBLINGS = 5
 ROUND_MAGIC = 1.5 * 2.0**23
@@ -38,9 +41,9 @@ FLOPS = 2 * P * B * 3 * WIDTH * WIDTH
 def turn_four_blocks(nc, banks, ident, block, grouped_words):
     bank = banks.tile([P, 2, 2, P], F32, tag="bank")
     for u in range(2):
-        for s in range(2):
-            nc.tensor.transpose(bank[:, u, s, :], block(u, s), ident[:])
-    nc.scalar.copy(out=grouped_words, in_=bank[:].rearrange("p u s r -> p (s r) u"))
+        for c in range(2):
+            nc.tensor.transpose(bank[:, u, c, :], block(u, c), ident[:])
+    nc.scalar.copy(out=grouped_words, in_=bank[:].rearrange("p u c r -> p c r u"))
 
 
 def tile_multiheadattention_pa_kernel(tc, x, in_proj_weight, in_proj_bias, out_0, out_1, out_2):
@@ -68,14 +71,18 @@ def tile_multiheadattention_pa_kernel(tc, x, in_proj_weight, in_proj_bias, out_0
 
         def load_weights(j):
             raw = w_pool.tile([P, 2, 2, WIDTH], BF16)
-            nc.sync.dma_start(out=raw[:], in_=w_tiles[order[j]])
+            if j < SPLIT_TILES:
+                for s in range(2):
+                    nc.sync.dma_start(out=raw[:, s], in_=w_tiles[order[j]][:, s])
+            else:
+                nc.sync.dma_start(out=raw[:], in_=w_tiles[order[j]])
             w_raw[j] = raw
 
-        bias_rows = const.tile([P, N_TILE], BF16)
-        nc.vector.memset(bias_rows[:], 0.0)
-        nc.sync.dma_start(out=bias_rows[0:N_TILES, :], in_=in_proj_bias.rearrange("(m c) -> m c", c=N_TILE))
         x_raw = const.tile([P, B, WIDTH], BF16)
         nc.sync.dma_start(out=x_raw[:], in_=x)
+        bias_rows = const.tile([P, 3 * WIDTH // BIAS_ROWS], BF16)
+        nc.vector.memset(bias_rows[:], 0.0)
+        nc.sync.dma_start(out=bias_rows[0:BIAS_ROWS, :], in_=in_proj_bias.rearrange("(m c) -> m c", m=BIAS_ROWS))
         for j in range(W_BUFS):
             load_weights(j)
 
@@ -128,18 +135,22 @@ def tile_multiheadattention_pa_kernel(tc, x, in_proj_weight, in_proj_bias, out_0
         cos = sin_cos[:, 1, :]
 
         bias_all = const.tile([P, 3 * WIDTH], BF16)
-        for pair in range(N_TILES // 2):
+        tiles_a_row = N_TILES // BIAS_ROWS
+
+        def spread_bias(pair):
             spread = banks.tile([P, 2 * N_TILE], BF16, tag="bank")
             for c in range(2):
-                m = 2 * pair + c
+                n = order[2 * pair + c]
+                m = n // tiles_a_row
                 nc.tensor.matmul(
                     out=spread[:, c * N_TILE : (c + 1) * N_TILE],
                     lhsT=ident_bf16[:, m : m + 1].to_broadcast([P, P]),
-                    rhs=bias_rows[:],
+                    rhs=bias_rows[:, (n % tiles_a_row) * N_TILE : (n % tiles_a_row + 1) * N_TILE],
                     start=True,
                     stop=True,
                 )
             nc.vector.tensor_copy(out=bias_all[:, 2 * pair * N_TILE : 2 * (pair + 1) * N_TILE], in_=spread[:])
+
         own_factor = const.tile([P, PAIRS, 2], F32)
         partner_factor = const.tile([P, PAIRS, 2], F32)
         nc.vector.tensor_copy(out=own_factor[:], in_=cos.unsqueeze(2).to_broadcast([P, PAIRS, 2]))
@@ -154,8 +165,10 @@ def tile_multiheadattention_pa_kernel(tc, x, in_proj_weight, in_proj_bias, out_0
                 banks,
                 ident,
                 lambda u, b: x_words[:, b, g * WORDS_PASS + u * P : g * WORDS_PASS + (u + 1) * P],
-                x_grouped[:, g].bitcast(F32),
+                x_grouped[:, g].bitcast(F32).rearrange("p (b r) u -> p b r u", b=B),
             )
+        for pair in range(EARLY_SPREADS):
+            spread_bias(pair)
         x_codes = const.tile([P, PASSES, B * P], U32, align_bytes=64)
         x_scales = const.tile([P, PASSES, B * P], U8, align_bytes=64)
         nc.vector.quantize_mx(
@@ -167,6 +180,22 @@ def tile_multiheadattention_pa_kernel(tc, x, in_proj_weight, in_proj_bias, out_0
         def turn_weights(j):
             w_words = w_raw[j][:].bitcast(F32)
             w_grouped[j] = []
+            if j < SPLIT_TILES:
+                for g in range(PASSES):
+                    grouped = grouped_pool.tile([P, N_TILE, 4], BF16, align_bytes=64)
+                    w_grouped[j].append(grouped)
+                for s in range(2):
+                    for g in range(PASSES):
+                        turn_four_blocks(
+                            nc,
+                            banks,
+                            ident,
+                            lambda u, e: w_words[:, s, e, g * WORDS_PASS + u * P : g * WORDS_PASS + (u + 1) * P],
+                            w_grouped[j][g][:].bitcast(F32).rearrange("p (e s r) u -> p e s r u", e=2, s=2)[:, :, s],
+                        )
+                    if EARLY_SPREADS + 2 * j + s < N_TILES // 2:
+                        spread_bias(EARLY_SPREADS + 2 * j + s)
+                return
             for g in range(PASSES):
                 grouped = grouped_pool.tile([P, N_TILE, 4], BF16, align_bytes=64)
                 for e in range(2):
@@ -175,7 +204,7 @@ def tile_multiheadattention_pa_kernel(tc, x, in_proj_weight, in_proj_bias, out_0
                         banks,
                         ident,
                         lambda u, s: w_words[:, s, e, g * WORDS_PASS + u * P : g * WORDS_PASS + (u + 1) * P],
-                        grouped[:].bitcast(F32)[:, e * 2 * P : (e + 1) * 2 * P, :],
+                        grouped[:].bitcast(F32).rearrange("p (e s r) u -> p e s r u", e=2, s=2)[:, e],
                     )
                 w_grouped[j].append(grouped)
 
@@ -209,7 +238,7 @@ def tile_multiheadattention_pa_kernel(tc, x, in_proj_weight, in_proj_bias, out_0
 
         def add_bias(j):
             n = order[j]
-            bias = bias_all[:, n * N_TILE : (n + 1) * N_TILE]
+            bias = bias_all[:, j * N_TILE : (j + 1) * N_TILE]
             result = out_pool.tile([P, B, TILE_HEADS, DH], F32)
             results[j] = result
             for b in range(B):

@@ -29,7 +29,7 @@ N_TILES = 3 * PART_TILES
 W_BUFS = 5
 GROUPED_BUFS = 8
 BIAS_ROWS = 4
-EARLY_SPREADS = 2
+EARLY_SPREADS = 3
 SPLIT_TILES = 3
 TURN_BANKS = 6
 DOUBLINGS = 5
@@ -78,11 +78,17 @@ def tile_multiheadattention_pa_kernel(tc, x, in_proj_weight, in_proj_bias, out_0
                 nc.sync.dma_start(out=raw[:], in_=w_tiles[order[j]])
             w_raw[j] = raw
 
-        x_raw = const.tile([P, B, WIDTH], BF16)
-        nc.sync.dma_start(out=x_raw[:], in_=x)
+        x_raw = []
         bias_rows = const.tile([P, 3 * WIDTH // BIAS_ROWS], BF16)
         nc.vector.memset(bias_rows[:], 0.0)
-        nc.sync.dma_start(out=bias_rows[0:BIAS_ROWS, :], in_=in_proj_bias.rearrange("(m c) -> m c", m=BIAS_ROWS))
+        for half in range(2):
+            x_half = const.tile([P, B, WIDTH // 2], BF16, tag="x_half%d" % half)
+            nc.sync.dma_start(out=x_half[:], in_=x[:, :, half * (WIDTH // 2) : (half + 1) * (WIDTH // 2)])
+            x_raw.append(x_half)
+            if half == 0:
+                nc.sync.dma_start(
+                    out=bias_rows[0:BIAS_ROWS, :], in_=in_proj_bias.rearrange("(m c) -> m c", m=BIAS_ROWS)
+                )
         for j in range(W_BUFS):
             load_weights(j)
 
@@ -157,17 +163,19 @@ def tile_multiheadattention_pa_kernel(tc, x, in_proj_weight, in_proj_bias, out_0
         nc.vector.tensor_scalar(out=partner_factor[:, :, 0], in0=sin, scalar1=-1.0, scalar2=None, op0=ALU.mult)
         nc.vector.tensor_copy(out=partner_factor[:, :, 1], in_=sin)
 
-        x_words = x_raw[:].bitcast(F32)
         x_grouped = const.tile([P, PASSES, B * P, 4], BF16, align_bytes=64)
         for g in range(PASSES):
+            x_words = x_raw[g // 2][:].bitcast(F32)
             turn_four_blocks(
                 nc,
                 banks,
                 ident,
-                lambda u, b: x_words[:, b, g * WORDS_PASS + u * P : g * WORDS_PASS + (u + 1) * P],
+                lambda u, b: x_words[:, b, (g % 2) * WORDS_PASS + u * P : (g % 2) * WORDS_PASS + (u + 1) * P],
                 x_grouped[:, g].bitcast(F32).rearrange("p (b r) u -> p b r u", b=B),
             )
-        for pair in range(EARLY_SPREADS):
+            if g == 1:
+                spread_bias(0)
+        for pair in range(1, EARLY_SPREADS):
             spread_bias(pair)
         x_codes = const.tile([P, PASSES, B * P], U32, align_bytes=64)
         x_scales = const.tile([P, PASSES, B * P], U8, align_bytes=64)
@@ -208,16 +216,17 @@ def tile_multiheadattention_pa_kernel(tc, x, in_proj_weight, in_proj_bias, out_0
                     )
                 w_grouped[j].append(grouped)
 
-        def quantise_weights(j):
-            codes = mx_pool.tile([P, PASSES, N_TILE], U32, align_bytes=64)
-            scales = mx_pool.tile([P, PASSES, N_TILE], U8, align_bytes=64)
-            for g in range(PASSES):
-                nc.vector.quantize_mx(
-                    out=codes[:, g, :].bitcast(FP8X4),
-                    scales=scales[:, g, :],
-                    in_=w_grouped[j][g][:].rearrange("p c t -> p (c t)"),
-                )
-            w_mx[j] = (codes, scales)
+        def quantise_weights(j, g):
+            if g == 0:
+                codes = mx_pool.tile([P, PASSES, N_TILE], U32, align_bytes=64)
+                scales = mx_pool.tile([P, PASSES, N_TILE], U8, align_bytes=64)
+                w_mx[j] = (codes, scales)
+            codes, scales = w_mx[j]
+            nc.vector.quantize_mx(
+                out=codes[:, g, :].bitcast(FP8X4),
+                scales=scales[:, g, :],
+                in_=w_grouped[j][g][:].rearrange("p c t -> p (c t)"),
+            )
 
         def multiply(j):
             codes, scales = w_mx[j]
@@ -236,18 +245,17 @@ def tile_multiheadattention_pa_kernel(tc, x, in_proj_weight, in_proj_bias, out_0
                     )
                 sums[j].append(total)
 
-        def add_bias(j):
-            n = order[j]
+        def add_bias(j, b):
             bias = bias_all[:, j * N_TILE : (j + 1) * N_TILE]
-            result = out_pool.tile([P, B, TILE_HEADS, DH], F32)
-            results[j] = result
-            for b in range(B):
-                nc.vector.tensor_tensor(
-                    out=result[:, b].rearrange("p h (i e) -> p (h i) e", e=2),
-                    in0=sums[j][b][:].rearrange("p (e c) -> p c e", e=2),
-                    in1=bias.rearrange("p (c e) -> p c e", e=2),
-                    op=ALU.add,
-                )
+            if b == 0:
+                result = out_pool.tile([P, B, TILE_HEADS, DH], F32)
+                results[j] = result
+            nc.vector.tensor_tensor(
+                out=results[j][:, b].rearrange("p h (i e) -> p (h i) e", e=2),
+                in0=sums[j][b][:].rearrange("p (e c) -> p c e", e=2),
+                in1=bias.rearrange("p (c e) -> p c e", e=2),
+                op=ALU.add,
+            )
 
         def rotate(j):
             if order[j] >= 2 * PART_TILES:
@@ -290,10 +298,15 @@ def tile_multiheadattention_pa_kernel(tc, x, in_proj_weight, in_proj_bias, out_0
                     load_weights(j + W_BUFS)
             if j > 0:
                 multiply(j - 1)
-            if j < N_TILES:
-                quantise_weights(j)
+            sums_after = [1, 2] if SPLIT_TILES <= j < N_TILES else [PASSES - 1, PASSES - 1]
+            for g in range(PASSES):
+                if j < N_TILES:
+                    quantise_weights(j, g)
+                if j > 0:
+                    for b in range(B):
+                        if sums_after[b] == g:
+                            add_bias(j - 1, b)
             if j > 0:
-                add_bias(j - 1)
                 rotate(j - 1)
                 waiting.append(j - 1)
                 if j + W_BUFS >= N_TILES - 1:

@@ -177,8 +177,8 @@ def tile_multiheadattention_pa_kernel(tc, x, in_proj_weight, in_proj_bias, out_0
                 spread_bias(0)
         for pair in range(1, EARLY_SPREADS):
             spread_bias(pair)
-        x_codes = const.tile([P, PASSES, B * P], U32, align_bytes=64)
-        x_scales = const.tile([P, PASSES, B * P], U8, align_bytes=64)
+        x_codes = const.tile([P, PASSES, B * P], U32, align_bytes=256)
+        x_scales = const.tile([P, PASSES, B * P], U8, align_bytes=256)
         nc.vector.quantize_mx(
             out=x_codes[:].rearrange("p g c -> p (g c)").bitcast(FP8X4),
             scales=x_scales[:].rearrange("p g c -> p (g c)"),
@@ -218,8 +218,8 @@ def tile_multiheadattention_pa_kernel(tc, x, in_proj_weight, in_proj_bias, out_0
 
         def quantise_weights(j, g):
             if g == 0:
-                codes = mx_pool.tile([P, PASSES, N_TILE], U32, align_bytes=64)
-                scales = mx_pool.tile([P, PASSES, N_TILE], U8, align_bytes=64)
+                codes = mx_pool.tile([P, PASSES, N_TILE], U32, align_bytes=256)
+                scales = mx_pool.tile([P, PASSES, N_TILE], U8, align_bytes=256)
                 w_mx[j] = (codes, scales)
             codes, scales = w_mx[j]
             nc.vector.quantize_mx(

@@ -28,10 +28,15 @@ PART_TILES = WIDTH // N_TILE
 N_TILES = 3 * PART_TILES
 W_BUFS = 5
 GROUPED_BUFS = 8
-BIAS_ROWS = 4
-EARLY_SPREADS = 3
+BIAS_ROWS = 32
+BIAS_COLS = 3 * WIDTH // BIAS_ROWS
+SPREAD_COLS = 2 * N_TILE
 SPLIT_TILES = 3
 TURN_BANKS = 6
+ROPE_BUFS = 2
+ROTATION_BACKLOG = 3
+EARLY_SPREADS = 2
+FIRST_LATE_SPREAD = EARLY_SPREADS + 1
 DOUBLINGS = 5
 ROUND_MAGIC = 1.5 * 2.0**23
 
@@ -49,7 +54,7 @@ def turn_four_blocks(nc, banks, ident, block, grouped_words):
 def tile_multiheadattention_pa_kernel(tc, x, in_proj_weight, in_proj_bias, out_0, out_1, out_2):
     nc = tc.nc
     outs = [out_0, out_1, out_2]
-    order = [part * PART_TILES + m for m in range(PART_TILES) for part in range(3)]
+    order = list(range(N_TILES))
     w_tiles = in_proj_weight.rearrange("(n s p e) k -> n p s e k", s=2, p=P, e=2)
 
     with ExitStack() as ctx:
@@ -58,7 +63,7 @@ def tile_multiheadattention_pa_kernel(tc, x, in_proj_weight, in_proj_bias, out_0
         w_pool = ctx.enter_context(tc.tile_pool(name="w_pool", bufs=W_BUFS))
         grouped_pool = ctx.enter_context(tc.tile_pool(name="grouped_pool", bufs=GROUPED_BUFS))
         mx_pool = ctx.enter_context(tc.tile_pool(name="mx_pool", bufs=2))
-        rope_pool = ctx.enter_context(tc.tile_pool(name="rope_pool", bufs=2))
+        rope_pool = ctx.enter_context(tc.tile_pool(name="rope_pool", bufs=ROPE_BUFS))
         out_pool = ctx.enter_context(tc.tile_pool(name="out_pool", bufs=N_TILES))
         banks = ctx.enter_context(tc.psum_pool(name="banks", bufs=TURN_BANKS))
         sums_pool = ctx.enter_context(tc.psum_pool(name="sums_pool", bufs=B))
@@ -79,16 +84,14 @@ def tile_multiheadattention_pa_kernel(tc, x, in_proj_weight, in_proj_bias, out_0
             w_raw[j] = raw
 
         x_raw = []
-        bias_rows = const.tile([P, 3 * WIDTH // BIAS_ROWS], BF16)
-        nc.vector.memset(bias_rows[:], 0.0)
+        bias_rows = const.tile([P, BIAS_COLS], BF16)
+        nc.sync.dma_start(out=bias_rows[0:BIAS_ROWS, :], in_=in_proj_bias.rearrange("(m c) -> m c", m=BIAS_ROWS))
+        nc.vector.memset(bias_rows[32:64, :], 0.0)
+        nc.vector.memset(bias_rows[64:128, :], 0.0)
         for half in range(2):
             x_half = const.tile([P, B, WIDTH // 2], BF16, tag="x_half%d" % half)
             nc.sync.dma_start(out=x_half[:], in_=x[:, :, half * (WIDTH // 2) : (half + 1) * (WIDTH // 2)])
             x_raw.append(x_half)
-            if half == 0:
-                nc.sync.dma_start(
-                    out=bias_rows[0:BIAS_ROWS, :], in_=in_proj_bias.rearrange("(m c) -> m c", m=BIAS_ROWS)
-                )
         for j in range(W_BUFS):
             load_weights(j)
 
@@ -141,21 +144,28 @@ def tile_multiheadattention_pa_kernel(tc, x, in_proj_weight, in_proj_bias, out_0
         cos = sin_cos[:, 1, :]
 
         bias_all = const.tile([P, 3 * WIDTH], BF16)
-        tiles_a_row = N_TILES // BIAS_ROWS
 
-        def spread_bias(pair):
-            spread = banks.tile([P, 2 * N_TILE], BF16, tag="bank")
-            for c in range(2):
-                n = order[2 * pair + c]
-                m = n // tiles_a_row
+        def spread_bias(part):
+            first = part * SPREAD_COLS
+            spread = banks.tile([P, SPREAD_COLS], BF16, tag="bank")
+            for m in range(first // BIAS_COLS, (first + SPREAD_COLS - 1) // BIAS_COLS + 1):
+                start = max(first, m * BIAS_COLS)
+                end = min(first + SPREAD_COLS, (m + 1) * BIAS_COLS)
                 nc.tensor.matmul(
-                    out=spread[:, c * N_TILE : (c + 1) * N_TILE],
+                    out=spread[:, start - first : end - first],
                     lhsT=ident_bf16[:, m : m + 1].to_broadcast([P, P]),
-                    rhs=bias_rows[:, (n % tiles_a_row) * N_TILE : (n % tiles_a_row + 1) * N_TILE],
+                    rhs=bias_rows[:, start - m * BIAS_COLS : end - m * BIAS_COLS],
                     start=True,
                     stop=True,
                 )
-            nc.vector.tensor_copy(out=bias_all[:, 2 * pair * N_TILE : 2 * (pair + 1) * N_TILE], in_=spread[:])
+
+            def keep():
+                nc.vector.tensor_copy(out=bias_all[:, first : first + SPREAD_COLS], in_=spread[:])
+
+            return keep
+
+        for part in range(EARLY_SPREADS):
+            spread_bias(part)()
 
         own_factor = const.tile([P, PAIRS, 2], F32)
         partner_factor = const.tile([P, PAIRS, 2], F32)
@@ -173,10 +183,7 @@ def tile_multiheadattention_pa_kernel(tc, x, in_proj_weight, in_proj_bias, out_0
                 lambda u, b: x_words[:, b, (g % 2) * WORDS_PASS + u * P : (g % 2) * WORDS_PASS + (u + 1) * P],
                 x_grouped[:, g].bitcast(F32).rearrange("p (b r) u -> p b r u", b=B),
             )
-            if g == 1:
-                spread_bias(0)
-        for pair in range(1, EARLY_SPREADS):
-            spread_bias(pair)
+        spread_bias(EARLY_SPREADS)()
         x_codes = const.tile([P, PASSES, B * P], U32, align_bytes=256)
         x_scales = const.tile([P, PASSES, B * P], U8, align_bytes=256)
         nc.vector.quantize_mx(
@@ -185,25 +192,25 @@ def tile_multiheadattention_pa_kernel(tc, x, in_proj_weight, in_proj_bias, out_0
             in_=x_grouped[:].rearrange("p g c t -> p (g c t)"),
         )
 
-        def turn_weights(j):
+        def turn_half(j, s):
             w_words = w_raw[j][:].bitcast(F32)
-            w_grouped[j] = []
-            if j < SPLIT_TILES:
+            if s == 0:
+                w_grouped[j] = []
                 for g in range(PASSES):
                     grouped = grouped_pool.tile([P, N_TILE, 4], BF16, align_bytes=64)
                     w_grouped[j].append(grouped)
-                for s in range(2):
-                    for g in range(PASSES):
-                        turn_four_blocks(
-                            nc,
-                            banks,
-                            ident,
-                            lambda u, e: w_words[:, s, e, g * WORDS_PASS + u * P : g * WORDS_PASS + (u + 1) * P],
-                            w_grouped[j][g][:].bitcast(F32).rearrange("p (e s r) u -> p e s r u", e=2, s=2)[:, :, s],
-                        )
-                    if EARLY_SPREADS + 2 * j + s < N_TILES // 2:
-                        spread_bias(EARLY_SPREADS + 2 * j + s)
-                return
+            for g in range(PASSES):
+                turn_four_blocks(
+                    nc,
+                    banks,
+                    ident,
+                    lambda u, e: w_words[:, s, e, g * WORDS_PASS + u * P : g * WORDS_PASS + (u + 1) * P],
+                    w_grouped[j][g][:].bitcast(F32).rearrange("p (s e r) u -> p s e r u", s=2, e=2)[:, s],
+                )
+
+        def turn_weights(j):
+            w_words = w_raw[j][:].bitcast(F32)
+            w_grouped[j] = []
             for g in range(PASSES):
                 grouped = grouped_pool.tile([P, N_TILE, 4], BF16, align_bytes=64)
                 for e in range(2):
@@ -212,104 +219,163 @@ def tile_multiheadattention_pa_kernel(tc, x, in_proj_weight, in_proj_bias, out_0
                         banks,
                         ident,
                         lambda u, s: w_words[:, s, e, g * WORDS_PASS + u * P : g * WORDS_PASS + (u + 1) * P],
-                        grouped[:].bitcast(F32).rearrange("p (e s r) u -> p e s r u", e=2, s=2)[:, e],
+                        grouped[:].bitcast(F32).rearrange("p (s e r) u -> p e s r u", s=2, e=2)[:, e],
                     )
                 w_grouped[j].append(grouped)
 
-        def quantise_weights(j, g):
-            if g == 0:
+        def quantise_weights(j, g, first=0, last=N_TILE):
+            if j not in w_mx:
                 codes = mx_pool.tile([P, PASSES, N_TILE], U32, align_bytes=256)
                 scales = mx_pool.tile([P, PASSES, N_TILE], U8, align_bytes=256)
                 w_mx[j] = (codes, scales)
             codes, scales = w_mx[j]
             nc.vector.quantize_mx(
-                out=codes[:, g, :].bitcast(FP8X4),
-                scales=scales[:, g, :],
-                in_=w_grouped[j][g][:].rearrange("p c t -> p (c t)"),
+                out=codes[:, g, first:last].bitcast(FP8X4),
+                scales=scales[:, g, first:last],
+                in_=w_grouped[j][g][:, first:last].rearrange("p c t -> p (c t)"),
             )
 
         def multiply(j):
             codes, scales = w_mx[j]
             sums[j] = []
             for b in range(B):
-                total = sums_pool.tile([P, N_TILE], F32)
-                for g in range(PASSES):
-                    nc.tensor.matmul_mx(
-                        out=total[:],
-                        lhsT=x_codes[:, g, b * P : (b + 1) * P].bitcast(FP8X4),
-                        lhsT_scale=x_scales[:, g, b * P : (b + 1) * P],
-                        rhs=codes[:, g, :].bitcast(FP8X4),
-                        rhs_scale=scales[:, g, :],
-                        start=(g == 0),
-                        stop=(g == PASSES - 1),
-                    )
+                if j < N_TILES - 1:
+                    total = sums_pool.tile([P, N_TILE], F32)
+                else:
+                    total = banks.tile([P, N_TILE], F32, tag="bank")
                 sums[j].append(total)
+            if j < N_TILES - 1:
+                passes = [(b, g) for b in range(B) for g in range(PASSES)]
+            else:
+                passes = [(b, g) for g in range(PASSES) for b in range(B)]
+            for b, g in passes:
+                nc.tensor.matmul_mx(
+                    out=sums[j][b][:],
+                    lhsT=x_codes[:, g, b * P : (b + 1) * P].bitcast(FP8X4),
+                    lhsT_scale=x_scales[:, g, b * P : (b + 1) * P],
+                    rhs=codes[:, g, :].bitcast(FP8X4),
+                    rhs_scale=scales[:, g, :],
+                    start=(g == 0),
+                    stop=(g == PASSES - 1),
+                )
 
         def add_bias(j, b):
-            bias = bias_all[:, j * N_TILE : (j + 1) * N_TILE]
+            bias = bias_all[:, order[j] * N_TILE : (order[j] + 1) * N_TILE]
             if b == 0:
                 result = out_pool.tile([P, B, TILE_HEADS, DH], F32)
                 results[j] = result
             nc.vector.tensor_tensor(
-                out=results[j][:, b].rearrange("p h (i e) -> p (h i) e", e=2),
-                in0=sums[j][b][:].rearrange("p (e c) -> p c e", e=2),
-                in1=bias.rearrange("p (c e) -> p c e", e=2),
+                out=results[j][:, b].rearrange("p (s h) (i e) -> p s (h i) e", s=2, e=2),
+                in0=sums[j][b][:].rearrange("p (s e c) -> p s c e", s=2, e=2),
+                in1=bias.rearrange("p (s c e) -> p s c e", s=2, e=2),
                 op=ALU.add,
             )
 
-        def rotate(j):
+        rotations = []
+        finished = []
+
+        def queue_rotation(j):
             if order[j] >= 2 * PART_TILES:
+                finished.append(j)
                 return
             rotated = results[j][:].rearrange("p b h d -> p (b h) d")[:, :, 0 : 2 * PAIRS]
             channels = rotated.rearrange("p c (i e) -> p c i e", e=2)
-            own = rope_pool.tile([P, B * TILE_HEADS, PAIRS, 2], F32)
-            partner = rope_pool.tile([P, B * TILE_HEADS, PAIRS, 2], F32)
-            nc.vector.tensor_tensor(
-                out=own[:],
-                in0=channels,
-                in1=own_factor[:].unsqueeze(1).to_broadcast([P, B * TILE_HEADS, PAIRS, 2]),
-                op=ALU.mult,
-            )
-            nc.vector.tensor_tensor(
-                out=partner[:],
-                in0=channels[:, :, :, ::-1],
-                in1=partner_factor[:].unsqueeze(1).to_broadcast([P, B * TILE_HEADS, PAIRS, 2]),
-                op=ALU.mult,
-            )
-            nc.vector.tensor_tensor(
-                out=rotated,
-                in0=own[:].rearrange("p c i e -> p c (i e)"),
-                in1=partner[:].rearrange("p c i e -> p c (i e)"),
-                op=ALU.add,
-            )
+            products = []
+
+            def multiply_own():
+                own = rope_pool.tile([P, B * TILE_HEADS, PAIRS, 2], F32)
+                products.append(own)
+                nc.vector.tensor_tensor(
+                    out=own[:],
+                    in0=channels,
+                    in1=own_factor[:].unsqueeze(1).to_broadcast([P, B * TILE_HEADS, PAIRS, 2]),
+                    op=ALU.mult,
+                )
+
+            def multiply_partner():
+                partner = rope_pool.tile([P, B * TILE_HEADS, PAIRS, 2], F32)
+                products.append(partner)
+                nc.vector.tensor_tensor(
+                    out=partner[:],
+                    in0=channels[:, :, :, ::-1],
+                    in1=partner_factor[:].unsqueeze(1).to_broadcast([P, B * TILE_HEADS, PAIRS, 2]),
+                    op=ALU.mult,
+                )
+
+            def add_products():
+                nc.vector.tensor_tensor(
+                    out=rotated,
+                    in0=products[0][:].rearrange("p c i e -> p c (i e)"),
+                    in1=products[1][:].rearrange("p c i e -> p c (i e)"),
+                    op=ALU.add,
+                )
+                finished.append(j)
+
+            rotations.extend([multiply_own, multiply_partner, add_products])
+
+        def rotate():
+            if len(rotations) > 0:
+                step = rotations[0]
+                rotations.remove(step)
+                step()
 
         def store(j):
             n = order[j]
             first_head = (n % PART_TILES) * TILE_HEADS
-            nc.sync.dma_start(
-                out=outs[n // PART_TILES][:, :, first_head : first_head + TILE_HEADS, :], in_=results[j][:]
-            )
+            if j < N_TILES - 1:
+                nc.sync.dma_start(
+                    out=outs[n // PART_TILES][:, :, first_head : first_head + TILE_HEADS, :], in_=results[j][:]
+                )
+            else:
+                for b in range(B):
+                    nc.sync.dma_start(
+                        out=outs[n // PART_TILES][:, b, first_head : first_head + TILE_HEADS, :], in_=results[j][:, b]
+                    )
 
-        waiting = []
         for j in range(N_TILES + 1):
-            if j < N_TILES:
+            keeps = []
+            if j < SPLIT_TILES:
+                for s in range(2):
+                    turn_half(j, s)
+                    part = FIRST_LATE_SPREAD + 2 * j + s
+                    if part < 3 * WIDTH // SPREAD_COLS:
+                        keeps.append(spread_bias(part))
+            elif j < N_TILES:
                 turn_weights(j)
-                if j + W_BUFS < N_TILES:
-                    load_weights(j + W_BUFS)
+            if j + W_BUFS < N_TILES:
+                load_weights(j + W_BUFS)
             if j > 0:
                 multiply(j - 1)
-            sums_after = [1, 2] if SPLIT_TILES <= j < N_TILES else [PASSES - 1, PASSES - 1]
-            for g in range(PASSES):
-                if j < N_TILES:
-                    quantise_weights(j, g)
-                if j > 0:
-                    for b in range(B):
-                        if sums_after[b] == g:
-                            add_bias(j - 1, b)
+            first = 0
+            if j < SPLIT_TILES:
+                rotate()
+                for g in range(PASSES):
+                    quantise_weights(j, g, 0, N_TILE // 2)
+                if len(keeps) > 0:
+                    keeps[0]()
+                first = N_TILE // 2
+                steps = ["turn", 0, 1, "add 0", 2, 3, "add 1"]
+            elif j < N_TILES - 1:
+                steps = ["turn", 0, "turn", 1, "add 0", 2, "add 1", 3]
+            elif j == N_TILES - 1:
+                steps = ["turn", 0, "turn", 1, "add 0", 2, 3, "add 1"]
+            else:
+                steps = ["turn", "turn", "add 0", "add 1"]
+            if SPLIT_TILES <= j < N_TILES and len(rotations) > ROTATION_BACKLOG:
+                rotate()
+            for step in steps:
+                if step == "turn":
+                    rotate()
+                elif step == "add 0" or step == "add 1":
+                    if j > 0:
+                        add_bias(j - 1, 0 if step == "add 0" else 1)
+                else:
+                    quantise_weights(j, step, first)
+            if len(keeps) > 1:
+                keeps[1]()
             if j > 0:
-                rotate(j - 1)
-                waiting.append(j - 1)
-                if j + W_BUFS >= N_TILES - 1:
-                    for finished in waiting:
-                        store(finished)
-                    waiting = []
+                queue_rotation(j - 1)
+            if j + W_BUFS >= N_TILES - 1:
+                for tile in finished:
+                    store(tile)
+                finished.clear()

@@ -28,15 +28,14 @@ PART_TILES = WIDTH // N_TILE
 N_TILES = 3 * PART_TILES
 W_BUFS = 5
 GROUPED_BUFS = 8
-BIAS_ROWS = 32
+BIAS_ROWS = 4
 BIAS_COLS = 3 * WIDTH // BIAS_ROWS
 SPREAD_COLS = 2 * N_TILE
 SPLIT_TILES = 3
 TURN_BANKS = 6
 ROPE_BUFS = 2
 ROTATION_BACKLOG = 3
-EARLY_SPREADS = 2
-FIRST_LATE_SPREAD = EARLY_SPREADS + 1
+EARLY_SPREADS = 3
 DOUBLINGS = 5
 ROUND_MAGIC = 1.5 * 2.0**23
 
@@ -85,13 +84,15 @@ def tile_multiheadattention_pa_kernel(tc, x, in_proj_weight, in_proj_bias, out_0
 
         x_raw = []
         bias_rows = const.tile([P, BIAS_COLS], BF16)
-        nc.sync.dma_start(out=bias_rows[0:BIAS_ROWS, :], in_=in_proj_bias.rearrange("(m c) -> m c", m=BIAS_ROWS))
-        nc.vector.memset(bias_rows[32:64, :], 0.0)
-        nc.vector.memset(bias_rows[64:128, :], 0.0)
+        nc.vector.memset(bias_rows[:], 0.0)
         for half in range(2):
             x_half = const.tile([P, B, WIDTH // 2], BF16, tag="x_half%d" % half)
             nc.sync.dma_start(out=x_half[:], in_=x[:, :, half * (WIDTH // 2) : (half + 1) * (WIDTH // 2)])
             x_raw.append(x_half)
+            if half == 0:
+                nc.sync.dma_start(
+                    out=bias_rows[0:BIAS_ROWS, :], in_=in_proj_bias.rearrange("(m c) -> m c", m=BIAS_ROWS)
+                )
         for j in range(W_BUFS):
             load_weights(j)
 
@@ -148,13 +149,12 @@ def tile_multiheadattention_pa_kernel(tc, x, in_proj_weight, in_proj_bias, out_0
         def spread_bias(part):
             first = part * SPREAD_COLS
             spread = banks.tile([P, SPREAD_COLS], BF16, tag="bank")
-            for m in range(first // BIAS_COLS, (first + SPREAD_COLS - 1) // BIAS_COLS + 1):
-                start = max(first, m * BIAS_COLS)
-                end = min(first + SPREAD_COLS, (m + 1) * BIAS_COLS)
+            for start in range(first, first + SPREAD_COLS, N_TILE):
+                m = start // BIAS_COLS
                 nc.tensor.matmul(
-                    out=spread[:, start - first : end - first],
+                    out=spread[:, start - first : start - first + N_TILE],
                     lhsT=ident_bf16[:, m : m + 1].to_broadcast([P, P]),
-                    rhs=bias_rows[:, start - m * BIAS_COLS : end - m * BIAS_COLS],
+                    rhs=bias_rows[:, start - m * BIAS_COLS : start - m * BIAS_COLS + N_TILE],
                     start=True,
                     stop=True,
                 )
@@ -164,8 +164,6 @@ def tile_multiheadattention_pa_kernel(tc, x, in_proj_weight, in_proj_bias, out_0
 
             return keep
 
-        for part in range(EARLY_SPREADS):
-            spread_bias(part)()
 
         own_factor = const.tile([P, PAIRS, 2], F32)
         partner_factor = const.tile([P, PAIRS, 2], F32)
@@ -183,7 +181,10 @@ def tile_multiheadattention_pa_kernel(tc, x, in_proj_weight, in_proj_bias, out_0
                 lambda u, b: x_words[:, b, (g % 2) * WORDS_PASS + u * P : (g % 2) * WORDS_PASS + (u + 1) * P],
                 x_grouped[:, g].bitcast(F32).rearrange("p (b r) u -> p b r u", b=B),
             )
-        spread_bias(EARLY_SPREADS)()
+            if g == 1:
+                spread_bias(0)()
+        for part in range(1, EARLY_SPREADS):
+            spread_bias(part)()
         x_codes = const.tile([P, PASSES, B * P], U32, align_bytes=256)
         x_scales = const.tile([P, PASSES, B * P], U8, align_bytes=256)
         nc.vector.quantize_mx(
@@ -337,7 +338,7 @@ def tile_multiheadattention_pa_kernel(tc, x, in_proj_weight, in_proj_bias, out_0
             if j < SPLIT_TILES:
                 for s in range(2):
                     turn_half(j, s)
-                    part = FIRST_LATE_SPREAD + 2 * j + s
+                    part = EARLY_SPREADS + 2 * j + s
                     if part < 3 * WIDTH // SPREAD_COLS:
                         keeps.append(spread_bias(part))
             elif j < N_TILES:

@@ -24,6 +24,7 @@ PASSES = WIDTH // K_PASS
 WORDS_PASS = K_PASS // 2
 N_TILE = 512
 TILE_HEADS = N_TILE // DH
+HALF_HEADS = TILE_HEADS // 2
 PART_TILES = WIDTH // N_TILE
 N_TILES = 3 * PART_TILES
 W_BUFS = 5
@@ -71,6 +72,7 @@ def tile_multiheadattention_pa_kernel(tc, x, in_proj_weight, in_proj_bias, out_0
         w_grouped = {}
         w_mx = {}
         sums = {}
+        half_sums = []
         results = {}
 
         def load_weights(j):
@@ -236,29 +238,32 @@ def tile_multiheadattention_pa_kernel(tc, x, in_proj_weight, in_proj_bias, out_0
                 in_=w_grouped[j][g][:, first:last].rearrange("p c t -> p (c t)"),
             )
 
-        def multiply(j):
+        def add_pass(total, j, b, g, first, last):
             codes, scales = w_mx[j]
+            nc.tensor.matmul_mx(
+                out=total,
+                lhsT=x_codes[:, g, b * P : (b + 1) * P].bitcast(FP8X4),
+                lhsT_scale=x_scales[:, g, b * P : (b + 1) * P],
+                rhs=codes[:, g, first:last].bitcast(FP8X4),
+                rhs_scale=scales[:, g, first:last],
+                start=(g == 0),
+                stop=(g == PASSES - 1),
+            )
+
+        def multiply(j):
             sums[j] = []
             for b in range(B):
-                if j < N_TILES - 1:
-                    total = sums_pool.tile([P, N_TILE], F32)
-                else:
-                    total = banks.tile([P, N_TILE], F32, tag="bank")
+                total = sums_pool.tile([P, N_TILE], F32)
                 sums[j].append(total)
-            if j < N_TILES - 1:
-                passes = [(b, g) for b in range(B) for g in range(PASSES)]
-            else:
-                passes = [(b, g) for g in range(PASSES) for b in range(B)]
-            for b, g in passes:
-                nc.tensor.matmul_mx(
-                    out=sums[j][b][:],
-                    lhsT=x_codes[:, g, b * P : (b + 1) * P].bitcast(FP8X4),
-                    lhsT_scale=x_scales[:, g, b * P : (b + 1) * P],
-                    rhs=codes[:, g, :].bitcast(FP8X4),
-                    rhs_scale=scales[:, g, :],
-                    start=(g == 0),
-                    stop=(g == PASSES - 1),
-                )
+                for g in range(PASSES):
+                    add_pass(total[:], j, b, g, 0, N_TILE)
+
+        def multiply_half(j, s):
+            total = banks.tile([P, B, N_TILE // 2], F32, tag="bank")
+            half_sums.append(total)
+            for b in range(B):
+                for g in range(PASSES):
+                    add_pass(total[:, b, :], j, b, g, s * (N_TILE // 2), (s + 1) * (N_TILE // 2))
 
         def add_bias(j, b):
             bias = bias_all[:, order[j] * N_TILE : (order[j] + 1) * N_TILE]
@@ -272,12 +277,23 @@ def tile_multiheadattention_pa_kernel(tc, x, in_proj_weight, in_proj_bias, out_0
                 op=ALU.add,
             )
 
+        def add_bias_half(j, s, b):
+            if j not in results:
+                result = out_pool.tile([P, B, TILE_HEADS, DH], F32)
+                results[j] = result
+            first = order[j] * N_TILE + s * (N_TILE // 2)
+            nc.vector.tensor_tensor(
+                out=results[j][:, b, s * HALF_HEADS : (s + 1) * HALF_HEADS].rearrange("p h (i e) -> p (h i) e", e=2),
+                in0=half_sums[s][:, b, :].rearrange("p (e c) -> p c e", e=2),
+                in1=bias_all[:, first : first + N_TILE // 2].rearrange("p (c e) -> p c e", e=2),
+                op=ALU.add,
+            )
+
         rotations = []
         finished = []
 
         def queue_rotation(j):
             if order[j] >= 2 * PART_TILES:
-                finished.append(j)
                 return
             rotated = results[j][:].rearrange("p b h d -> p (b h) d")[:, :, 0 : 2 * PAIRS]
             channels = rotated.rearrange("p c (i e) -> p c i e", e=2)
@@ -320,35 +336,31 @@ def tile_multiheadattention_pa_kernel(tc, x, in_proj_weight, in_proj_bias, out_0
                 rotations.remove(step)
                 step()
 
-        def store(j):
+        def store(j, b, first, last):
             n = order[j]
             first_head = (n % PART_TILES) * TILE_HEADS
-            if j < N_TILES - 1:
-                nc.sync.dma_start(
-                    out=outs[n // PART_TILES][:, :, first_head : first_head + TILE_HEADS, :], in_=results[j][:]
-                )
-            else:
-                for b in range(B):
-                    nc.sync.dma_start(
-                        out=outs[n // PART_TILES][:, b, first_head : first_head + TILE_HEADS, :], in_=results[j][:, b]
-                    )
+            nc.sync.dma_start(
+                out=outs[n // PART_TILES][:, b, first_head + first : first_head + last, :],
+                in_=results[j][:, b, first:last],
+            )
 
-        for j in range(N_TILES + 1):
+        for j in range(N_TILES):
             keeps = []
-            if j < SPLIT_TILES:
+            halved = j < SPLIT_TILES or j == N_TILES - 1
+            if halved:
                 for s in range(2):
                     turn_half(j, s)
                     part = EARLY_SPREADS + 2 * j + s
                     if part < 3 * WIDTH // SPREAD_COLS:
                         keeps.append(spread_bias(part))
-            elif j < N_TILES:
+            else:
                 turn_weights(j)
             if j + W_BUFS < N_TILES:
                 load_weights(j + W_BUFS)
             if j > 0:
                 multiply(j - 1)
             first = 0
-            if j < SPLIT_TILES:
+            if halved:
                 rotate()
                 for g in range(PASSES):
                     quantise_weights(j, g, 0, N_TILE // 2)
@@ -356,20 +368,19 @@ def tile_multiheadattention_pa_kernel(tc, x, in_proj_weight, in_proj_bias, out_0
                     keeps[0]()
                 first = N_TILE // 2
                 steps = ["turn", 0, 1, "add 0", 2, 3, "add 1"]
-            elif j < N_TILES - 1:
-                steps = ["turn", 0, "turn", 1, "add 0", 2, "add 1", 3]
-            elif j == N_TILES - 1:
-                steps = ["turn", 0, "turn", 1, "add 0", 2, 3, "add 1"]
             else:
-                steps = ["turn", "turn", "add 0", "add 1"]
-            if SPLIT_TILES <= j < N_TILES and len(rotations) > ROTATION_BACKLOG:
+                steps = ["turn", 0, "turn", 1, "add 0", 2, "add 1", 3]
+            if SPLIT_TILES <= j and len(rotations) > ROTATION_BACKLOG:
                 rotate()
             for step in steps:
                 if step == "turn":
                     rotate()
                 elif step == "add 0" or step == "add 1":
                     if j > 0:
-                        add_bias(j - 1, 0 if step == "add 0" else 1)
+                        b = 0 if step == "add 0" else 1
+                        add_bias(j - 1, b)
+                        if order[j - 1] >= 2 * PART_TILES:
+                            store(j - 1, slice(b, b + 1), 0, TILE_HEADS)
                 else:
                     quantise_weights(j, step, first)
             if len(keeps) > 1:
@@ -378,5 +389,13 @@ def tile_multiheadattention_pa_kernel(tc, x, in_proj_weight, in_proj_bias, out_0
                 queue_rotation(j - 1)
             if j + W_BUFS >= N_TILES - 1:
                 for tile in finished:
-                    store(tile)
+                    store(tile, slice(0, B), 0, TILE_HEADS)
                 finished.clear()
+
+        last = N_TILES - 1
+        for s in range(2):
+            multiply_half(last, s)
+        for s in range(2):
+            for b in range(B):
+                add_bias_half(last, s, b)
+                store(last, slice(b, b + 1), s * HALF_HEADS, (s + 1) * HALF_HEADS)

@@ -37,6 +37,7 @@ TURN_BANKS = 6
 ROPE_BUFS = 2
 ROTATION_BACKLOG = 3
 EARLY_SPREADS = 3
+X_LOADS = [[0,1],[1,1],[2,2]]
 DOUBLINGS = 5
 ROUND_MAGIC = 1.5 * 2.0**23
 
@@ -72,7 +73,7 @@ def tile_multiheadattention_pa_kernel(tc, x, in_proj_weight, in_proj_bias, out_0
         w_grouped = {}
         w_mx = {}
         sums = {}
-        half_sums = []
+        half_sums = {}
         results = {}
 
         def load_weights(j):
@@ -87,11 +88,12 @@ def tile_multiheadattention_pa_kernel(tc, x, in_proj_weight, in_proj_bias, out_0
         x_raw = []
         bias_rows = const.tile([P, BIAS_COLS], BF16)
         nc.vector.memset(bias_rows[:], 0.0)
-        for half in range(2):
-            x_half = const.tile([P, B, WIDTH // 2], BF16, tag="x_half%d" % half)
-            nc.sync.dma_start(out=x_half[:], in_=x[:, :, half * (WIDTH // 2) : (half + 1) * (WIDTH // 2)])
-            x_raw.append(x_half)
-            if half == 0:
+        for first, count in X_LOADS:
+            x_part = const.tile([P, B, count * K_PASS], BF16, tag="x_part%d" % first)
+            nc.sync.dma_start(out=x_part[:], in_=x[:, :, first * K_PASS : (first + count) * K_PASS])
+            for g in range(count):
+                x_raw.append(x_part[:, :, g * K_PASS : (g + 1) * K_PASS])
+            if first + count == 2:
                 nc.sync.dma_start(
                     out=bias_rows[0:BIAS_ROWS, :], in_=in_proj_bias.rearrange("(m c) -> m c", m=BIAS_ROWS)
                 )
@@ -175,12 +177,12 @@ def tile_multiheadattention_pa_kernel(tc, x, in_proj_weight, in_proj_bias, out_0
 
         x_grouped = const.tile([P, PASSES, B * P, 4], BF16, align_bytes=64)
         for g in range(PASSES):
-            x_words = x_raw[g // 2][:].bitcast(F32)
+            x_words = x_raw[g].bitcast(F32)
             turn_four_blocks(
                 nc,
                 banks,
                 ident,
-                lambda u, b: x_words[:, b, (g % 2) * WORDS_PASS + u * P : (g % 2) * WORDS_PASS + (u + 1) * P],
+                lambda u, b: x_words[:, b, u * P : (u + 1) * P],
                 x_grouped[:, g].bitcast(F32).rearrange("p (b r) u -> p b r u", b=B),
             )
             if g == 1:
@@ -259,11 +261,11 @@ def tile_multiheadattention_pa_kernel(tc, x, in_proj_weight, in_proj_bias, out_0
                     add_pass(total[:], j, b, g, 0, N_TILE)
 
         def multiply_half(j, s):
-            total = banks.tile([P, B, N_TILE // 2], F32, tag="bank")
-            half_sums.append(total)
             for b in range(B):
+                total = banks.tile([P, N_TILE // 2], F32, tag="bank")
+                half_sums[s, b] = total
                 for g in range(PASSES):
-                    add_pass(total[:, b, :], j, b, g, s * (N_TILE // 2), (s + 1) * (N_TILE // 2))
+                    add_pass(total[:], j, b, g, s * (N_TILE // 2), (s + 1) * (N_TILE // 2))
 
         def add_bias(j, b):
             bias = bias_all[:, order[j] * N_TILE : (order[j] + 1) * N_TILE]
@@ -284,7 +286,7 @@ def tile_multiheadattention_pa_kernel(tc, x, in_proj_weight, in_proj_bias, out_0
             first = order[j] * N_TILE + s * (N_TILE // 2)
             nc.vector.tensor_tensor(
                 out=results[j][:, b, s * HALF_HEADS : (s + 1) * HALF_HEADS].rearrange("p h (i e) -> p (h i) e", e=2),
-                in0=half_sums[s][:, b, :].rearrange("p (e c) -> p c e", e=2),
+                in0=half_sums[s, b][:].rearrange("p (e c) -> p c e", e=2),
                 in1=bias_all[:, first : first + N_TILE // 2].rearrange("p (c e) -> p c e", e=2),
                 op=ALU.add,
             )
@@ -364,8 +366,8 @@ def tile_multiheadattention_pa_kernel(tc, x, in_proj_weight, in_proj_bias, out_0
                 rotate()
                 for g in range(PASSES):
                     quantise_weights(j, g, 0, N_TILE // 2)
-                if len(keeps) > 0:
-                    keeps[0]()
+                    if g == 1 and len(keeps) > 0:
+                        keeps[0]()
                 first = N_TILE // 2
                 steps = ["turn", 0, 1, "add 0", 2, 3, "add 1"]
             else:
@@ -383,8 +385,8 @@ def tile_multiheadattention_pa_kernel(tc, x, in_proj_weight, in_proj_bias, out_0
                             store(j - 1, slice(b, b + 1), 0, TILE_HEADS)
                 else:
                     quantise_weights(j, step, first)
-            if len(keeps) > 1:
-                keeps[1]()
+                    if step == 1 and len(keeps) > 1:
+                        keeps[1]()
             if j > 0:
                 queue_rotation(j - 1)
             if j + W_BUFS >= N_TILES - 1:

@@ -29,14 +29,14 @@ PART_TILES = WIDTH // N_TILE
 N_TILES = 3 * PART_TILES
 W_BUFS = 5
 GROUPED_BUFS = 8
-BIAS_ROWS = 4
-BIAS_COLS = 3 * WIDTH // BIAS_ROWS
-SPREAD_COLS = 2 * N_TILE
+QUADRANT = 32
+BIAS_WORDS = 3 * WIDTH // 2
+BIAS_ROW_WORDS = BIAS_WORDS // QUADRANT
+BIAS_CHUNKS = 4
 SPLIT_TILES = 3
 TURN_BANKS = 6
 ROPE_BUFS = 2
 ROTATION_BACKLOG = 3
-EARLY_SPREADS = 3
 X_LOADS = [[0,1],[1,1],[2,2]]
 DOUBLINGS = 5
 ROUND_MAGIC = 1.5 * 2.0**23
@@ -86,17 +86,18 @@ def tile_multiheadattention_pa_kernel(tc, x, in_proj_weight, in_proj_bias, out_0
             w_raw[j] = raw
 
         x_raw = []
-        bias_rows = const.tile([P, BIAS_COLS], BF16)
-        nc.vector.memset(bias_rows[:], 0.0)
+        bias_rows = const.tile([P, 2 * BIAS_ROW_WORDS], BF16, align_bytes=64)
         for first, count in X_LOADS:
             x_part = const.tile([P, B, count * K_PASS], BF16, tag="x_part%d" % first)
             nc.sync.dma_start(out=x_part[:], in_=x[:, :, first * K_PASS : (first + count) * K_PASS])
             for g in range(count):
                 x_raw.append(x_part[:, :, g * K_PASS : (g + 1) * K_PASS])
-            if first + count == 2:
-                nc.sync.dma_start(
-                    out=bias_rows[0:BIAS_ROWS, :], in_=in_proj_bias.rearrange("(m c) -> m c", m=BIAS_ROWS)
-                )
+            if first == 0:
+                for quadrant in range(0, P, QUADRANT):
+                    nc.sync.dma_start(
+                        out=bias_rows[quadrant : quadrant + QUADRANT, :],
+                        in_=in_proj_bias.rearrange("(i c) -> i c", i=QUADRANT),
+                    )
         for j in range(W_BUFS):
             load_weights(j)
 
@@ -118,8 +119,6 @@ def tile_multiheadattention_pa_kernel(tc, x, in_proj_weight, in_proj_bias, out_0
             )
         position = const.tile([P, 1], F32)
         nc.vector.tensor_copy(out=position[:], in_=position_int[:])
-        ident_bf16 = const.tile([P, P], BF16)
-        nc.vector.tensor_copy(out=ident_bf16[:], in_=ident[:])
         turns = const.tile([P, 2, PAIRS], F32)
         nc.vector.tensor_scalar(
             out=turns[:, 0, :],
@@ -148,27 +147,34 @@ def tile_multiheadattention_pa_kernel(tc, x, in_proj_weight, in_proj_bias, out_0
         sin = sin_cos[:, 0, :]
         cos = sin_cos[:, 1, :]
 
-        bias_all = const.tile([P, 3 * WIDTH], BF16)
+        bias_turned = const.tile([P, BIAS_ROW_WORDS], F32, align_bytes=64)
+        for b in range(0, BIAS_ROW_WORDS, QUADRANT):
+            nc.vector.transpose(
+                out=bias_turned[:, b : b + QUADRANT], in_=bias_rows[:].bitcast(F32)[:, b : b + QUADRANT]
+            )
+        bias_repeated = const.tile([P, BIAS_WORDS], F32, align_bytes=64)
+        bias_words = const.tile([P, BIAS_WORDS], F32, align_bytes=64)
+        bias_all = bias_words[:].bitcast(BF16)
+        chunk_rows = QUADRANT // BIAS_CHUNKS
+        chunk_words = BIAS_WORDS // BIAS_CHUNKS
 
-        def spread_bias(part):
-            first = part * SPREAD_COLS
-            spread = banks.tile([P, SPREAD_COLS], BF16, tag="bank")
-            for start in range(first, first + SPREAD_COLS, N_TILE):
-                m = start // BIAS_COLS
-                nc.tensor.matmul(
-                    out=spread[:, start - first : start - first + N_TILE],
-                    lhsT=ident_bf16[:, m : m + 1].to_broadcast([P, P]),
-                    rhs=bias_rows[:, start - m * BIAS_COLS : start - m * BIAS_COLS + N_TILE],
-                    start=True,
-                    stop=True,
-                )
+        def repeat_bias(chunk):
+            nc.vector.tensor_copy(
+                out=bias_repeated[:, chunk * chunk_words : (chunk + 1) * chunk_words].rearrange(
+                    "p (i b k) -> p i b k", i=chunk_rows, k=QUADRANT
+                ),
+                in_=bias_turned[:]
+                .rearrange("p (b i) -> p i b", i=QUADRANT)[:, chunk * chunk_rows : (chunk + 1) * chunk_rows, :]
+                .unsqueeze(3)
+                .to_broadcast([P, chunk_rows, BIAS_ROW_WORDS // QUADRANT, QUADRANT]),
+            )
 
-            def keep():
-                nc.vector.tensor_copy(out=bias_all[:, first : first + SPREAD_COLS], in_=spread[:])
+        def turn_bias(chunk):
+            words = slice(chunk * chunk_words, (chunk + 1) * chunk_words)
+            nc.vector.transpose(out=bias_words[:, words], in_=bias_repeated[:, words])
 
-            return keep
-
-
+        for chunk in range(4):
+            repeat_bias(chunk)
         own_factor = const.tile([P, PAIRS, 2], F32)
         partner_factor = const.tile([P, PAIRS, 2], F32)
         nc.vector.tensor_copy(out=own_factor[:], in_=cos.unsqueeze(2).to_broadcast([P, PAIRS, 2]))
@@ -185,10 +191,8 @@ def tile_multiheadattention_pa_kernel(tc, x, in_proj_weight, in_proj_bias, out_0
                 lambda u, b: x_words[:, b, u * P : (u + 1) * P],
                 x_grouped[:, g].bitcast(F32).rearrange("p (b r) u -> p b r u", b=B),
             )
-            if g == 1:
-                spread_bias(0)()
-        for part in range(1, EARLY_SPREADS):
-            spread_bias(part)()
+        for chunk in range(4):
+            turn_bias(chunk)
         x_codes = const.tile([P, PASSES, B * P], U32, align_bytes=256)
         x_scales = const.tile([P, PASSES, B * P], U8, align_bytes=256)
         nc.vector.quantize_mx(
@@ -347,14 +351,10 @@ def tile_multiheadattention_pa_kernel(tc, x, in_proj_weight, in_proj_bias, out_0
             )
 
         for j in range(N_TILES):
-            keeps = []
             halved = j < SPLIT_TILES or j == N_TILES - 1
             if halved:
                 for s in range(2):
                     turn_half(j, s)
-                    part = EARLY_SPREADS + 2 * j + s
-                    if part < 3 * WIDTH // SPREAD_COLS:
-                        keeps.append(spread_bias(part))
             else:
                 turn_weights(j)
             if j + W_BUFS < N_TILES:
@@ -366,8 +366,10 @@ def tile_multiheadattention_pa_kernel(tc, x, in_proj_weight, in_proj_bias, out_0
                 rotate()
                 for g in range(PASSES):
                     quantise_weights(j, g, 0, N_TILE // 2)
-                    if g == 1 and len(keeps) > 0:
-                        keeps[0]()
+                    if g == 0 and j + 4 < BIAS_CHUNKS:
+                        repeat_bias(j + 4)
+                    if g == 2 and j + 4 < BIAS_CHUNKS:
+                        turn_bias(j + 4)
                 first = N_TILE // 2
                 steps = ["turn", 0, 1, "add 0", 2, 3, "add 1"]
             else:
@@ -385,8 +387,6 @@ def tile_multiheadattention_pa_kernel(tc, x, in_proj_weight, in_proj_bias, out_0
                             store(j - 1, slice(b, b + 1), 0, TILE_HEADS)
                 else:
                     quantise_weights(j, step, first)
-                    if step == 1 and len(keeps) > 1:
-                        keeps[1]()
             if j > 0:
                 queue_rotation(j - 1)
             if j + W_BUFS >= N_TILES - 1:

@@ -36,7 +36,6 @@ BIAS_CHUNKS = 4
 SPLIT_TILES = 3
 TURN_BANKS = 6
 ROPE_BUFS = 2
-ROTATION_BACKLOG = 3
 X_LOADS = [[0,1],[1,1],[2,2]]
 DOUBLINGS = 5
 ROUND_MAGIC = 1.5 * 2.0**23
@@ -295,52 +294,32 @@ def tile_multiheadattention_pa_kernel(tc, x, in_proj_weight, in_proj_bias, out_0
                 op=ALU.add,
             )
 
-        rotations = []
         finished = []
 
-        def queue_rotation(j):
-            if order[j] >= 2 * PART_TILES:
-                return
+        def rotate(j):
             rotated = results[j][:].rearrange("p b h d -> p (b h) d")[:, :, 0 : 2 * PAIRS]
             channels = rotated.rearrange("p c (i e) -> p c i e", e=2)
-            products = []
-
-            def multiply_own():
-                own = rope_pool.tile([P, B * TILE_HEADS, PAIRS, 2], F32)
-                products.append(own)
-                nc.vector.tensor_tensor(
-                    out=own[:],
-                    in0=channels,
-                    in1=own_factor[:].unsqueeze(1).to_broadcast([P, B * TILE_HEADS, PAIRS, 2]),
-                    op=ALU.mult,
-                )
-
-            def multiply_partner():
-                partner = rope_pool.tile([P, B * TILE_HEADS, PAIRS, 2], F32)
-                products.append(partner)
-                nc.vector.tensor_tensor(
-                    out=partner[:],
-                    in0=channels[:, :, :, ::-1],
-                    in1=partner_factor[:].unsqueeze(1).to_broadcast([P, B * TILE_HEADS, PAIRS, 2]),
-                    op=ALU.mult,
-                )
-
-            def add_products():
-                nc.vector.tensor_tensor(
-                    out=rotated,
-                    in0=products[0][:].rearrange("p c i e -> p c (i e)"),
-                    in1=products[1][:].rearrange("p c i e -> p c (i e)"),
-                    op=ALU.add,
-                )
-                finished.append(j)
-
-            rotations.extend([multiply_own, multiply_partner, add_products])
-
-        def rotate():
-            if len(rotations) > 0:
-                step = rotations[0]
-                rotations.remove(step)
-                step()
+            own = rope_pool.tile([P, B * TILE_HEADS, PAIRS, 2], F32)
+            partner = rope_pool.tile([P, B * TILE_HEADS, PAIRS, 2], F32)
+            nc.vector.tensor_tensor(
+                out=own[:],
+                in0=channels,
+                in1=own_factor[:].unsqueeze(1).to_broadcast([P, B * TILE_HEADS, PAIRS, 2]),
+                op=ALU.mult,
+            )
+            nc.vector.tensor_tensor(
+                out=partner[:],
+                in0=channels[:, :, :, ::-1],
+                in1=partner_factor[:].unsqueeze(1).to_broadcast([P, B * TILE_HEADS, PAIRS, 2]),
+                op=ALU.mult,
+            )
+            nc.gpsimd.tensor_tensor(
+                out=rotated,
+                in0=own[:].rearrange("p c i e -> p c (i e)"),
+                in1=partner[:].rearrange("p c i e -> p c (i e)"),
+                op=ALU.add,
+            )
+            finished.append(j)
 
         def store(j, b, first, last):
             n = order[j]
@@ -363,22 +342,17 @@ def tile_multiheadattention_pa_kernel(tc, x, in_proj_weight, in_proj_bias, out_0
                 multiply(j - 1)
             first = 0
             if halved:
-                rotate()
                 for g in range(PASSES):
                     quantise_weights(j, g, 0, N_TILE // 2)
-                    if g == 0 and j + 4 < BIAS_CHUNKS:
-                        repeat_bias(j + 4)
-                    if g == 2 and j + 4 < BIAS_CHUNKS:
-                        turn_bias(j + 4)
                 first = N_TILE // 2
-                steps = ["turn", 0, 1, "add 0", 2, 3, "add 1"]
+                steps = [0, 1, "add 0", 2, 3, "add 1"]
             else:
-                steps = ["turn", 0, "turn", 1, "add 0", 2, "add 1", 3]
-            if SPLIT_TILES <= j and len(rotations) > ROTATION_BACKLOG:
-                rotate()
+                steps = [0, 1, "add 0", 2, "add 1", 3]
+            if 0 <= j - 2 < 2 * PART_TILES:
+                steps = [0, 1, "rotate", "add 0", "add 1", 2, 3]
             for step in steps:
-                if step == "turn":
-                    rotate()
+                if step == "rotate":
+                    rotate(j - 2)
                 elif step == "add 0" or step == "add 1":
                     if j > 0:
                         b = 0 if step == "add 0" else 1
@@ -387,8 +361,6 @@ def tile_multiheadattention_pa_kernel(tc, x, in_proj_weight, in_proj_bias, out_0
                             store(j - 1, slice(b, b + 1), 0, TILE_HEADS)
                 else:
                     quantise_weights(j, step, first)
-            if j > 0:
-                queue_rotation(j - 1)
             if j + W_BUFS >= N_TILES - 1:
                 for tile in finished:
                     store(tile, slice(0, B), 0, TILE_HEADS)

@@ -33,10 +33,10 @@ QUADRANT = 32
 BIAS_WORDS = 3 * WIDTH // 2
 BIAS_ROW_WORDS = BIAS_WORDS // QUADRANT
 BIAS_CHUNKS = 4
-SPLIT_TILES = 3
+SPLIT_TILES = 4
 TURN_BANKS = 6
 ROPE_BUFS = 2
-X_LOADS = [[0,1],[1,1],[2,2]]
+PAIR_TILES = 2
 DOUBLINGS = 5
 ROUND_MAGIC = 1.5 * 2.0**23
 
@@ -54,7 +54,6 @@ def turn_four_blocks(nc, banks, ident, block, grouped_words):
 def tile_multiheadattention_pa_kernel(tc, x, in_proj_weight, in_proj_bias, out_0, out_1, out_2):
     nc = tc.nc
     outs = [out_0, out_1, out_2]
-    order = list(range(N_TILES))
     w_tiles = in_proj_weight.rearrange("(n s p e) k -> n p s e k", s=2, p=P, e=2)
 
     with ExitStack() as ctx:
@@ -64,7 +63,7 @@ def tile_multiheadattention_pa_kernel(tc, x, in_proj_weight, in_proj_bias, out_0
         grouped_pool = ctx.enter_context(tc.tile_pool(name="grouped_pool", bufs=GROUPED_BUFS))
         mx_pool = ctx.enter_context(tc.tile_pool(name="mx_pool", bufs=2))
         rope_pool = ctx.enter_context(tc.tile_pool(name="rope_pool", bufs=ROPE_BUFS))
-        out_pool = ctx.enter_context(tc.tile_pool(name="out_pool", bufs=N_TILES))
+        out_pool = ctx.enter_context(tc.tile_pool(name="out_pool", bufs=B * N_TILES // PAIR_TILES))
         banks = ctx.enter_context(tc.psum_pool(name="banks", bufs=TURN_BANKS))
         sums_pool = ctx.enter_context(tc.psum_pool(name="sums_pool", bufs=B))
 
@@ -73,30 +72,29 @@ def tile_multiheadattention_pa_kernel(tc, x, in_proj_weight, in_proj_bias, out_0
         w_mx = {}
         sums = {}
         half_sums = {}
-        results = {}
+        pair_results = {}
 
         def load_weights(j):
             raw = w_pool.tile([P, 2, 2, WIDTH], BF16)
             if j < SPLIT_TILES:
                 for s in range(2):
-                    nc.sync.dma_start(out=raw[:, s], in_=w_tiles[order[j]][:, s])
+                    nc.sync.dma_start(out=raw[:, s], in_=w_tiles[j][:, s])
             else:
-                nc.sync.dma_start(out=raw[:], in_=w_tiles[order[j]])
+                nc.sync.dma_start(out=raw[:], in_=w_tiles[j])
             w_raw[j] = raw
 
         x_raw = []
-        bias_rows = const.tile([P, 2 * BIAS_ROW_WORDS], BF16, align_bytes=64)
-        for first, count in X_LOADS:
-            x_part = const.tile([P, B, count * K_PASS], BF16, tag="x_part%d" % first)
-            nc.sync.dma_start(out=x_part[:], in_=x[:, :, first * K_PASS : (first + count) * K_PASS])
-            for g in range(count):
-                x_raw.append(x_part[:, :, g * K_PASS : (g + 1) * K_PASS])
-            if first == 0:
-                for quadrant in range(0, P, QUADRANT):
-                    nc.sync.dma_start(
-                        out=bias_rows[quadrant : quadrant + QUADRANT, :],
-                        in_=in_proj_bias.rearrange("(i c) -> i c", i=QUADRANT),
-                    )
+        bias_rows = const.tile([P, 2 * BIAS_ROW_WORDS], BF16)
+        nc.vector.memset(bias_rows[32:64, :], 0.0)
+        nc.vector.memset(bias_rows[64:128, :], 0.0)
+        for b in range(B):
+            x_entry = const.tile([P, WIDTH], BF16, tag="x_entry%d" % b)
+            nc.sync.dma_start(out=x_entry[:], in_=x[:, b, :])
+            x_raw.append(x_entry)
+            if b == 0:
+                nc.sync.dma_start(
+                    out=bias_rows[0:QUADRANT, :], in_=in_proj_bias.rearrange("(i c) -> i c", i=QUADRANT)
+                )
         for j in range(W_BUFS):
             load_weights(j)
 
@@ -146,16 +144,32 @@ def tile_multiheadattention_pa_kernel(tc, x, in_proj_weight, in_proj_bias, out_0
         sin = sin_cos[:, 0, :]
         cos = sin_cos[:, 1, :]
 
+        quadrants = const.tile([P, P // QUADRANT, QUADRANT], BF16)
+        nc.vector.tensor_copy(
+            out=quadrants[:], in_=ident[:, 0:QUADRANT].unsqueeze(1).to_broadcast([P, P // QUADRANT, QUADRANT])
+        )
+        bias_quads = const.tile([P, 2 * BIAS_ROW_WORDS], BF16, align_bytes=64)
         bias_turned = const.tile([P, BIAS_ROW_WORDS], F32, align_bytes=64)
-        for b in range(0, BIAS_ROW_WORDS, QUADRANT):
-            nc.vector.transpose(
-                out=bias_turned[:, b : b + QUADRANT], in_=bias_rows[:].bitcast(F32)[:, b : b + QUADRANT]
-            )
         bias_repeated = const.tile([P, BIAS_WORDS], F32, align_bytes=64)
         bias_words = const.tile([P, BIAS_WORDS], F32, align_bytes=64)
         bias_all = bias_words[:].bitcast(BF16)
         chunk_rows = QUADRANT // BIAS_CHUNKS
         chunk_words = BIAS_WORDS // BIAS_CHUNKS
+
+        def copy_bias_rows():
+            copies = banks.tile([P, 2 * BIAS_ROW_WORDS], BF16, tag="bank")
+            nc.tensor.matmul(
+                out=copies[:],
+                lhsT=quadrants[:].rearrange("p q i -> p (q i)"),
+                rhs=bias_rows[:],
+                start=True,
+                stop=True,
+            )
+            nc.vector.tensor_copy(out=bias_quads[:], in_=copies[:])
+            for b in range(0, BIAS_ROW_WORDS, QUADRANT):
+                nc.vector.transpose(
+                    out=bias_turned[:, b : b + QUADRANT], in_=bias_quads[:].bitcast(F32)[:, b : b + QUADRANT]
+                )
 
         def repeat_bias(chunk):
             nc.vector.tensor_copy(
@@ -172,8 +186,6 @@ def tile_multiheadattention_pa_kernel(tc, x, in_proj_weight, in_proj_bias, out_0
             words = slice(chunk * chunk_words, (chunk + 1) * chunk_words)
             nc.vector.transpose(out=bias_words[:, words], in_=bias_repeated[:, words])
 
-        for chunk in range(4):
-            repeat_bias(chunk)
         own_factor = const.tile([P, PAIRS, 2], F32)
         partner_factor = const.tile([P, PAIRS, 2], F32)
         nc.vector.tensor_copy(out=own_factor[:], in_=cos.unsqueeze(2).to_broadcast([P, PAIRS, 2]))
@@ -181,16 +193,21 @@ def tile_multiheadattention_pa_kernel(tc, x, in_proj_weight, in_proj_bias, out_0
         nc.vector.tensor_copy(out=partner_factor[:, :, 1], in_=sin)
 
         x_grouped = const.tile([P, PASSES, B * P, 4], BF16, align_bytes=64)
-        for g in range(PASSES):
-            x_words = x_raw[g].bitcast(F32)
-            turn_four_blocks(
-                nc,
-                banks,
-                ident,
-                lambda u, b: x_words[:, b, u * P : (u + 1) * P],
-                x_grouped[:, g].bitcast(F32).rearrange("p (b r) u -> p b r u", b=B),
-            )
-        for chunk in range(4):
+        for b in range(B):
+            x_words = x_raw[b][:].bitcast(F32)
+            for pair in range(0, PASSES, 2):
+                turn_four_blocks(
+                    nc,
+                    banks,
+                    ident,
+                    lambda u, c: x_words[:, (pair + c) * WORDS_PASS + u * P : (pair + c) * WORDS_PASS + (u + 1) * P],
+                    x_grouped[:, pair : pair + 2, b * P : (b + 1) * P, :].bitcast(F32),
+                )
+            if b == 0:
+                copy_bias_rows()
+                for chunk in range(BIAS_CHUNKS):
+                    repeat_bias(chunk)
+        for chunk in range(BIAS_CHUNKS):
             turn_bias(chunk)
         x_codes = const.tile([P, PASSES, B * P], U32, align_bytes=256)
         x_scales = const.tile([P, PASSES, B * P], U8, align_bytes=256)
@@ -270,65 +287,64 @@ def tile_multiheadattention_pa_kernel(tc, x, in_proj_weight, in_proj_bias, out_0
                 for g in range(PASSES):
                     add_pass(total[:], j, b, g, s * (N_TILE // 2), (s + 1) * (N_TILE // 2))
 
+        def result(j, b):
+            pair, m = divmod(j, PAIR_TILES)
+            if (pair, b) not in pair_results:
+                both = out_pool.tile([P, PAIR_TILES * TILE_HEADS, DH], F32)
+                pair_results[pair, b] = both
+            return pair_results[pair, b][:, m * TILE_HEADS : (m + 1) * TILE_HEADS, :]
+
         def add_bias(j, b):
-            bias = bias_all[:, order[j] * N_TILE : (order[j] + 1) * N_TILE]
-            if b == 0:
-                result = out_pool.tile([P, B, TILE_HEADS, DH], F32)
-                results[j] = result
+            bias = bias_all[:, j * N_TILE : (j + 1) * N_TILE]
             nc.vector.tensor_tensor(
-                out=results[j][:, b].rearrange("p (s h) (i e) -> p s (h i) e", s=2, e=2),
+                out=result(j, b).rearrange("p (s h) (i e) -> p s (h i) e", s=2, e=2),
                 in0=sums[j][b][:].rearrange("p (s e c) -> p s c e", s=2, e=2),
                 in1=bias.rearrange("p (s c e) -> p s c e", s=2, e=2),
                 op=ALU.add,
             )
 
         def add_bias_half(j, s, b):
-            if j not in results:
-                result = out_pool.tile([P, B, TILE_HEADS, DH], F32)
-                results[j] = result
-            first = order[j] * N_TILE + s * (N_TILE // 2)
+            first = j * N_TILE + s * (N_TILE // 2)
             nc.vector.tensor_tensor(
-                out=results[j][:, b, s * HALF_HEADS : (s + 1) * HALF_HEADS].rearrange("p h (i e) -> p (h i) e", e=2),
+                out=result(j, b)[:, s * HALF_HEADS : (s + 1) * HALF_HEADS].rearrange("p h (i e) -> p (h i) e", e=2),
                 in0=half_sums[s, b][:].rearrange("p (e c) -> p c e", e=2),
                 in1=bias_all[:, first : first + N_TILE // 2].rearrange("p (c e) -> p c e", e=2),
                 op=ALU.add,
             )
 
-        finished = []
-
         def rotate(j):
-            rotated = results[j][:].rearrange("p b h d -> p (b h) d")[:, :, 0 : 2 * PAIRS]
-            channels = rotated.rearrange("p c (i e) -> p c i e", e=2)
-            own = rope_pool.tile([P, B * TILE_HEADS, PAIRS, 2], F32)
-            partner = rope_pool.tile([P, B * TILE_HEADS, PAIRS, 2], F32)
-            nc.vector.tensor_tensor(
-                out=own[:],
-                in0=channels,
-                in1=own_factor[:].unsqueeze(1).to_broadcast([P, B * TILE_HEADS, PAIRS, 2]),
-                op=ALU.mult,
-            )
-            nc.vector.tensor_tensor(
-                out=partner[:],
-                in0=channels[:, :, :, ::-1],
-                in1=partner_factor[:].unsqueeze(1).to_broadcast([P, B * TILE_HEADS, PAIRS, 2]),
-                op=ALU.mult,
-            )
-            nc.gpsimd.tensor_tensor(
-                out=rotated,
-                in0=own[:].rearrange("p c i e -> p c (i e)"),
-                in1=partner[:].rearrange("p c i e -> p c (i e)"),
-                op=ALU.add,
-            )
-            finished.append(j)
+            rotated = [result(j, b)[:, :, 0 : 2 * PAIRS] for b in range(B)]
+            own = rope_pool.tile([P, B, TILE_HEADS, 2 * PAIRS], F32)
+            partner = rope_pool.tile([P, B, TILE_HEADS, 2 * PAIRS], F32)
+            for b in range(B):
+                nc.vector.tensor_tensor(
+                    out=own[:, b],
+                    in0=rotated[b],
+                    in1=own_factor[:]
+                    .rearrange("p i e -> p (i e)")
+                    .unsqueeze(1)
+                    .to_broadcast([P, TILE_HEADS, 2 * PAIRS]),
+                    op=ALU.mult,
+                )
+            for b in range(B):
+                nc.vector.tensor_tensor(
+                    out=partner[:, b].rearrange("p h (i e) -> p h i e", e=2),
+                    in0=rotated[b].rearrange("p h (i e) -> p h i e", e=2)[:, :, :, ::-1],
+                    in1=partner_factor[:].unsqueeze(1).to_broadcast([P, TILE_HEADS, PAIRS, 2]),
+                    op=ALU.mult,
+                )
+            for b in range(B):
+                nc.gpsimd.tensor_tensor(out=rotated[b], in0=own[:, b], in1=partner[:, b], op=ALU.add)
 
         def store(j, b, first, last):
-            n = order[j]
-            first_head = (n % PART_TILES) * TILE_HEADS
+            first_head = (j % PART_TILES) * TILE_HEADS
+            pair, m = divmod(j, PAIR_TILES)
             nc.sync.dma_start(
-                out=outs[n // PART_TILES][:, b, first_head + first : first_head + last, :],
-                in_=results[j][:, b, first:last],
+                out=outs[j // PART_TILES][:, b, first_head + first : first_head + last, :],
+                in_=pair_results[pair, b][:, m * TILE_HEADS + first : m * TILE_HEADS + last, :],
             )
 
+        stored = 0
         for j in range(N_TILES):
             halved = j < SPLIT_TILES or j == N_TILES - 1
             if halved:
@@ -357,14 +373,16 @@ def tile_multiheadattention_pa_kernel(tc, x, in_proj_weight, in_proj_bias, out_0
                     if j > 0:
                         b = 0 if step == "add 0" else 1
                         add_bias(j - 1, b)
-                        if order[j - 1] >= 2 * PART_TILES:
-                            store(j - 1, slice(b, b + 1), 0, TILE_HEADS)
+                        if j - 1 >= 2 * PART_TILES:
+                            store(j - 1, b, 0, TILE_HEADS)
                 else:
                     quantise_weights(j, step, first)
             if j + W_BUFS >= N_TILES - 1:
-                for tile in finished:
-                    store(tile, slice(0, B), 0, TILE_HEADS)
-                finished.clear()
+                ready = min((j - 1) // PAIR_TILES, 2 * PART_TILES // PAIR_TILES)
+                for pair in range(stored, ready):
+                    for b in range(B):
+                        store(pair * PAIR_TILES, b, 0, PAIR_TILES * TILE_HEADS)
+                stored = max(stored, ready)
 
         last = N_TILES - 1
         for s in range(2):
@@ -372,4 +390,4 @@ def tile_multiheadattention_pa_kernel(tc, x, in_proj_weight, in_proj_bias, out_0
         for s in range(2):
             for b in range(B):
                 add_bias_half(last, s, b)
-                store(last, slice(b, b + 1), s * HALF_HEADS, (s + 1) * HALF_HEADS)
+                store(last, b, s * HALF_HEADS, (s + 1) * HALF_HEADS)

import math
from contextlib import ExitStack

import concourse.mybir as mybir
from concourse.masks import make_identity

F32 = mybir.dt.float32
BF16 = mybir.dt.bfloat16
I32 = mybir.dt.int32
U32 = mybir.dt.uint32
U8 = mybir.dt.uint8
FP8X4 = mybir.dt.float8_e4m3fn_x4
ALU = mybir.AluOpType

P = 128
B = 2
HEADS = 16
DH = 128
WIDTH = HEADS * DH
PAIRS = 32
FIRST_POSITION = 512 - 128
K_PASS = 4 * P
PASSES = WIDTH // K_PASS
WORDS_PASS = K_PASS // 2
N_TILE = 512
TILE_HEADS = N_TILE // DH
HALF_HEADS = TILE_HEADS // 2
PART_TILES = WIDTH // N_TILE
N_TILES = 3 * PART_TILES
W_BUFS = 5
GROUPED_BUFS = 8
QUADRANT = 32
BIAS_WORDS = 3 * WIDTH // 2
BIAS_ROW_WORDS = BIAS_WORDS // QUADRANT
BIAS_CHUNKS = 4
SPLIT_TILES = 4
TURN_BANKS = 6
ROPE_BUFS = 2
PAIR_TILES = 2
DOUBLINGS = 5
ROUND_MAGIC = 1.5 * 2.0**23

FLOPS = 2 * P * B * 3 * WIDTH * WIDTH


def turn_four_blocks(nc, banks, ident, block, grouped_words):
    bank = banks.tile([P, 2, 2, P], F32, tag="bank")
    for u in range(2):
        for c in range(2):
            nc.tensor.transpose(bank[:, u, c, :], block(u, c), ident[:])
    nc.scalar.copy(out=grouped_words, in_=bank[:].rearrange("p u c r -> p c r u"))


def tile_multiheadattention_pa_kernel(tc, x, in_proj_weight, in_proj_bias, out_0, out_1, out_2):
    nc = tc.nc
    outs = [out_0, out_1, out_2]
    w_tiles = in_proj_weight.rearrange("(n s p e) k -> n p s e k", s=2, p=P, e=2)

    with ExitStack() as ctx:
        ctx.enter_context(tc.manual_schedule())
        const = ctx.enter_context(tc.tile_pool(name="const", bufs=1))
        w_pool = ctx.enter_context(tc.tile_pool(name="w_pool", bufs=W_BUFS))
        grouped_pool = ctx.enter_context(tc.tile_pool(name="grouped_pool", bufs=GROUPED_BUFS))
        mx_pool = ctx.enter_context(tc.tile_pool(name="mx_pool", bufs=2))
        rope_pool = ctx.enter_context(tc.tile_pool(name="rope_pool", bufs=ROPE_BUFS))
        out_pool = ctx.enter_context(tc.tile_pool(name="out_pool", bufs=B * N_TILES // PAIR_TILES))
        banks = ctx.enter_context(tc.psum_pool(name="banks", bufs=TURN_BANKS))
        sums_pool = ctx.enter_context(tc.psum_pool(name="sums_pool", bufs=B))

        w_raw = {}
        w_grouped = {}
        w_mx = {}
        sums = {}
        half_sums = {}
        pair_results = {}

        def load_weights(j):
            raw = w_pool.tile([P, 2, 2, WIDTH], BF16)
            if j < SPLIT_TILES:
                for s in range(2):
                    nc.sync.dma_start(out=raw[:, s], in_=w_tiles[j][:, s])
            else:
                nc.sync.dma_start(out=raw[:], in_=w_tiles[j])
            w_raw[j] = raw

        x_raw = []
        bias_rows = const.tile([P, 2 * BIAS_ROW_WORDS], BF16)
        nc.vector.memset(bias_rows[32:64, :], 0.0)
        nc.vector.memset(bias_rows[64:128, :], 0.0)
        for b in range(B):
            x_entry = const.tile([P, WIDTH], BF16, tag="x_entry%d" % b)
            nc.sync.dma_start(out=x_entry[:], in_=x[:, b, :])
            x_raw.append(x_entry)
            if b == 0:
                nc.sync.dma_start(
                    out=bias_rows[0:QUADRANT, :], in_=in_proj_bias.rearrange("(i c) -> i c", i=QUADRANT)
                )
        for j in range(W_BUFS):
            load_weights(j)

        position_int = const.tile([P, 1], I32)
        nc.gpsimd.iota(position_int[:], pattern=[[0, 1]], base=FIRST_POSITION, channel_multiplier=1)
        ident = const.tile([P, P], F32)
        make_identity(nc, ident[:])

        frequency = const.tile([P, PAIRS], F32)
        nc.vector.memset(frequency[:, 0:1], 1.0)
        for level in range(DOUBLINGS):
            run = 2**level
            nc.vector.tensor_scalar(
                out=frequency[:, run : 2 * run],
                in0=frequency[:, 0:run],
                scalar1=10000.0 ** (-2.0 * run / (2 * PAIRS)),
                scalar2=None,
                op0=ALU.mult,
            )
        position = const.tile([P, 1], F32)
        nc.vector.tensor_copy(out=position[:], in_=position_int[:])
        turns = const.tile([P, 2, PAIRS], F32)
        nc.vector.tensor_scalar(
            out=turns[:, 0, :],
            in0=frequency[:],
            scalar1=position[:, 0:1],
            scalar2=1.0 / (2.0 * math.pi),
            op0=ALU.mult,
            op1=ALU.mult,
        )
        nc.vector.tensor_scalar(out=turns[:, 1, :], in0=turns[:, 0, :], scalar1=0.25, scalar2=None, op0=ALU.add)
        whole_turns = const.tile([P, 2, PAIRS], F32)
        nc.vector.tensor_scalar(
            out=whole_turns[:],
            in0=turns[:],
            scalar1=ROUND_MAGIC,
            scalar2=ROUND_MAGIC,
            op0=ALU.add,
            op1=ALU.subtract,
        )
        part_turns = const.tile([P, 2, PAIRS], F32)
        nc.vector.tensor_tensor(out=part_turns[:], in0=turns[:], in1=whole_turns[:], op=ALU.subtract)
        sin_cos = const.tile([P, 2, PAIRS], F32)
        nc.scalar.activation(
            out=sin_cos[:], in_=part_turns[:], func=mybir.ActivationFunctionType.Sin, scale=2.0 * math.pi
        )
        sin = sin_cos[:, 0, :]
        cos = sin_cos[:, 1, :]

        quadrants = const.tile([P, P // QUADRANT, QUADRANT], BF16)
        nc.vector.tensor_copy(
            out=quadrants[:], in_=ident[:, 0:QUADRANT].unsqueeze(1).to_broadcast([P, P // QUADRANT, QUADRANT])
        )
        bias_quads = const.tile([P, 2 * BIAS_ROW_WORDS], BF16, align_bytes=64)
        bias_turned = const.tile([P, BIAS_ROW_WORDS], F32, align_bytes=64)
        bias_repeated = const.tile([P, BIAS_WORDS], F32, align_bytes=64)
        bias_words = const.tile([P, BIAS_WORDS], F32, align_bytes=64)
        bias_all = bias_words[:].bitcast(BF16)
        chunk_rows = QUADRANT // BIAS_CHUNKS
        chunk_words = BIAS_WORDS // BIAS_CHUNKS

        def copy_bias_rows():
            copies = banks.tile([P, 2 * BIAS_ROW_WORDS], BF16, tag="bank")
            nc.tensor.matmul(
                out=copies[:],
                lhsT=quadrants[:].rearrange("p q i -> p (q i)"),
                rhs=bias_rows[:],
                start=True,
                stop=True,
            )
            nc.vector.tensor_copy(out=bias_quads[:], in_=copies[:])
            for b in range(0, BIAS_ROW_WORDS, QUADRANT):
                nc.vector.transpose(
                    out=bias_turned[:, b : b + QUADRANT], in_=bias_quads[:].bitcast(F32)[:, b : b + QUADRANT]
                )

        def repeat_bias(chunk):
            nc.vector.tensor_copy(
                out=bias_repeated[:, chunk * chunk_words : (chunk + 1) * chunk_words].rearrange(
                    "p (i b k) -> p i b k", i=chunk_rows, k=QUADRANT
                ),
                in_=bias_turned[:]
                .rearrange("p (b i) -> p i b", i=QUADRANT)[:, chunk * chunk_rows : (chunk + 1) * chunk_rows, :]
                .unsqueeze(3)
                .to_broadcast([P, chunk_rows, BIAS_ROW_WORDS // QUADRANT, QUADRANT]),
            )

        def turn_bias(chunk):
            words = slice(chunk * chunk_words, (chunk + 1) * chunk_words)
            nc.vector.transpose(out=bias_words[:, words], in_=bias_repeated[:, words])

        own_factor = const.tile([P, PAIRS, 2], F32)
        partner_factor = const.tile([P, PAIRS, 2], F32)
        nc.vector.tensor_copy(out=own_factor[:], in_=cos.unsqueeze(2).to_broadcast([P, PAIRS, 2]))
        nc.vector.tensor_scalar(out=partner_factor[:, :, 0], in0=sin, scalar1=-1.0, scalar2=None, op0=ALU.mult)
        nc.vector.tensor_copy(out=partner_factor[:, :, 1], in_=sin)

        x_grouped = const.tile([P, PASSES, B * P, 4], BF16, align_bytes=64)
        for b in range(B):
            x_words = x_raw[b][:].bitcast(F32)
            for pair in range(0, PASSES, 2):
                turn_four_blocks(
                    nc,
                    banks,
                    ident,
                    lambda u, c: x_words[:, (pair + c) * WORDS_PASS + u * P : (pair + c) * WORDS_PASS + (u + 1) * P],
                    x_grouped[:, pair : pair + 2, b * P : (b + 1) * P, :].bitcast(F32),
                )
            if b == 0:
                copy_bias_rows()
                for chunk in range(BIAS_CHUNKS):
                    repeat_bias(chunk)
        for chunk in range(BIAS_CHUNKS):
            turn_bias(chunk)
        x_codes = const.tile([P, PASSES, B * P], U32, align_bytes=256)
        x_scales = const.tile([P, PASSES, B * P], U8, align_bytes=256)
        nc.vector.quantize_mx(
            out=x_codes[:].rearrange("p g c -> p (g c)").bitcast(FP8X4),
            scales=x_scales[:].rearrange("p g c -> p (g c)"),
            in_=x_grouped[:].rearrange("p g c t -> p (g c t)"),
        )

        def turn_half(j, s):
            w_words = w_raw[j][:].bitcast(F32)
            if s == 0:
                w_grouped[j] = []
                for g in range(PASSES):
                    grouped = grouped_pool.tile([P, N_TILE, 4], BF16, align_bytes=64)
                    w_grouped[j].append(grouped)
            for g in range(PASSES):
                turn_four_blocks(
                    nc,
                    banks,
                    ident,
                    lambda u, e: w_words[:, s, e, g * WORDS_PASS + u * P : g * WORDS_PASS + (u + 1) * P],
                    w_grouped[j][g][:].bitcast(F32).rearrange("p (s e r) u -> p s e r u", s=2, e=2)[:, s],
                )

        def turn_weights(j):
            w_words = w_raw[j][:].bitcast(F32)
            w_grouped[j] = []
            for g in range(PASSES):
                grouped = grouped_pool.tile([P, N_TILE, 4], BF16, align_bytes=64)
                for e in range(2):
                    turn_four_blocks(
                        nc,
                        banks,
                        ident,
                        lambda u, s: w_words[:, s, e, g * WORDS_PASS + u * P : g * WORDS_PASS + (u + 1) * P],
                        grouped[:].bitcast(F32).rearrange("p (s e r) u -> p e s r u", s=2, e=2)[:, e],
                    )
                w_grouped[j].append(grouped)

        def quantise_weights(j, g, first=0, last=N_TILE):
            if j not in w_mx:
                codes = mx_pool.tile([P, PASSES, N_TILE], U32, align_bytes=256)
                scales = mx_pool.tile([P, PASSES, N_TILE], U8, align_bytes=256)
                w_mx[j] = (codes, scales)
            codes, scales = w_mx[j]
            nc.vector.quantize_mx(
                out=codes[:, g, first:last].bitcast(FP8X4),
                scales=scales[:, g, first:last],
                in_=w_grouped[j][g][:, first:last].rearrange("p c t -> p (c t)"),
            )

        def add_pass(total, j, b, g, first, last):
            codes, scales = w_mx[j]
            nc.tensor.matmul_mx(
                out=total,
                lhsT=x_codes[:, g, b * P : (b + 1) * P].bitcast(FP8X4),
                lhsT_scale=x_scales[:, g, b * P : (b + 1) * P],
                rhs=codes[:, g, first:last].bitcast(FP8X4),
                rhs_scale=scales[:, g, first:last],
                start=(g == 0),
                stop=(g == PASSES - 1),
            )

        def multiply(j):
            sums[j] = []
            for b in range(B):
                total = sums_pool.tile([P, N_TILE], F32)
                sums[j].append(total)
                for g in range(PASSES):
                    add_pass(total[:], j, b, g, 0, N_TILE)

        def multiply_half(j, s):
            for b in range(B):
                total = banks.tile([P, N_TILE // 2], F32, tag="bank")
                half_sums[s, b] = total
                for g in range(PASSES):
                    add_pass(total[:], j, b, g, s * (N_TILE // 2), (s + 1) * (N_TILE // 2))

        def result(j, b):
            pair, m = divmod(j, PAIR_TILES)
            if (pair, b) not in pair_results:
                both = out_pool.tile([P, PAIR_TILES * TILE_HEADS, DH], F32)
                pair_results[pair, b] = both
            return pair_results[pair, b][:, m * TILE_HEADS : (m + 1) * TILE_HEADS, :]

        def add_bias(j, b):
            bias = bias_all[:, j * N_TILE : (j + 1) * N_TILE]
            nc.vector.tensor_tensor(
                out=result(j, b).rearrange("p (s h) (i e) -> p s (h i) e", s=2, e=2),
                in0=sums[j][b][:].rearrange("p (s e c) -> p s c e", s=2, e=2),
                in1=bias.rearrange("p (s c e) -> p s c e", s=2, e=2),
                op=ALU.add,
            )

        def add_bias_half(j, s, b):
            first = j * N_TILE + s * (N_TILE // 2)
            nc.vector.tensor_tensor(
                out=result(j, b)[:, s * HALF_HEADS : (s + 1) * HALF_HEADS].rearrange("p h (i e) -> p (h i) e", e=2),
                in0=half_sums[s, b][:].rearrange("p (e c) -> p c e", e=2),
                in1=bias_all[:, first : first + N_TILE // 2].rearrange("p (c e) -> p c e", e=2),
                op=ALU.add,
            )

        def rotate(j):
            rotated = [result(j, b)[:, :, 0 : 2 * PAIRS] for b in range(B)]
            own = rope_pool.tile([P, B, TILE_HEADS, 2 * PAIRS], F32)
            partner = rope_pool.tile([P, B, TILE_HEADS, 2 * PAIRS], F32)
            for b in range(B):
                nc.vector.tensor_tensor(
                    out=own[:, b],
                    in0=rotated[b],
                    in1=own_factor[:]
                    .rearrange("p i e -> p (i e)")
                    .unsqueeze(1)
                    .to_broadcast([P, TILE_HEADS, 2 * PAIRS]),
                    op=ALU.mult,
                )
            for b in range(B):
                nc.vector.tensor_tensor(
                    out=partner[:, b].rearrange("p h (i e) -> p h i e", e=2),
                    in0=rotated[b].rearrange("p h (i e) -> p h i e", e=2)[:, :, :, ::-1],
                    in1=partner_factor[:].unsqueeze(1).to_broadcast([P, TILE_HEADS, PAIRS, 2]),
                    op=ALU.mult,
                )
            for b in range(B):
                nc.gpsimd.tensor_tensor(out=rotated[b], in0=own[:, b], in1=partner[:, b], op=ALU.add)

        def store(j, b, first, last):
            first_head = (j % PART_TILES) * TILE_HEADS
            pair, m = divmod(j, PAIR_TILES)
            nc.sync.dma_start(
                out=outs[j // PART_TILES][:, b, first_head + first : first_head + last, :],
                in_=pair_results[pair, b][:, m * TILE_HEADS + first : m * TILE_HEADS + last, :],
            )

        stored = 0
        for j in range(N_TILES):
            halved = j < SPLIT_TILES or j == N_TILES - 1
            if halved:
                for s in range(2):
                    turn_half(j, s)
            else:
                turn_weights(j)
            if j + W_BUFS < N_TILES:
                load_weights(j + W_BUFS)
            if j > 0:
                multiply(j - 1)
            first = 0
            if halved:
                for g in range(PASSES):
                    quantise_weights(j, g, 0, N_TILE // 2)
                first = N_TILE // 2
                steps = [0, 1, "add 0", 2, 3, "add 1"]
            else:
                steps = [0, 1, "add 0", 2, "add 1", 3]
            if 0 <= j - 2 < 2 * PART_TILES:
                steps = [0, 1, "rotate", "add 0", "add 1", 2, 3]
            for step in steps:
                if step == "rotate":
                    rotate(j - 2)
                elif step == "add 0" or step == "add 1":
                    if j > 0:
                        b = 0 if step == "add 0" else 1
                        add_bias(j - 1, b)
                        if j - 1 >= 2 * PART_TILES:
                            store(j - 1, b, 0, TILE_HEADS)
                else:
                    quantise_weights(j, step, first)
            if j + W_BUFS >= N_TILES - 1:
                ready = min((j - 1) // PAIR_TILES, 2 * PART_TILES // PAIR_TILES)
                for pair in range(stored, ready):
                    for b in range(B):
                        store(pair * PAIR_TILES, b, 0, PAIR_TILES * TILE_HEADS)
                stored = max(stored, ready)

        last = N_TILES - 1
        for s in range(2):
            multiply_half(last, s)
        for s in range(2):
            for b in range(B):
                add_bias_half(last, s, b)
                store(last, b, s * HALF_HEADS, (s + 1) * HALF_HEADS)
